import numpy as np
import ml_dtypes


def mxq(x, axis, fmt="e4m3"):
    dtype, down = {"e4m3": (ml_dtypes.float8_e4m3fn, 7), "e5m2": (ml_dtypes.float8_e5m2, 14)}[fmt]
    v = np.moveaxis(np.asarray(x, np.float32).astype(ml_dtypes.bfloat16).astype(np.float64), axis, -1)
    blocks = v.reshape(v.shape[:-1] + (-1, 32))
    amax = np.abs(blocks).max(-1, keepdims=True)
    byte = np.maximum(np.where(amax > 0, np.frexp(amax)[1] - 1 + 127, 0) - down, 1)
    scale = np.exp2(byte - 127.0)
    codes = (blocks / scale).astype(np.float32).astype(dtype).astype(np.float64)
    return np.moveaxis((codes * scale).reshape(v.shape), -1, axis)


WIDE = False


def mx_kscale(k):
    if not WIDE:
        return np.ones(k)
    levels = np.array([10, -10, 5, -5, 0])
    a = np.random.permutation(np.resize(levels, k // 512 * 4)).reshape(k // 512, 4)
    idx = np.arange(k)
    return np.exp2(a[idx // 512, idx % 128 // 32])


BF16 = ml_dtypes.bfloat16


def bf(x):
    return np.asarray(x, np.float32).astype(BF16)


def f64(x):
    return np.asarray(x).astype(np.float64)


B, N, C, E = 4, 1024, 256, 1024
EPS_NORM = 1e-12


def setup_inputs():
    t = mx_kscale(E)
    g = np.random.standard_normal((B, N, E)) ** 2
    cm = np.sqrt((1.0 + 0.01 * N) / 3.0)
    kv = 0.8 * np.random.standard_normal((B, E, E)) + cm * np.random.standard_normal((B, 1, E))
    return {"q_feat": bf(g / g.sum(axis=2, keepdims=True)),
            "kv": bf(kv * t),
            "v": bf(np.random.standard_normal((B, N, E)) * t),
            "w_proj": bf(np.random.standard_normal((E, C)) / np.sqrt(E) / t[:, None]),
            "b_proj": bf(0.2 * np.random.standard_normal(C))}


def reference(q_feat, kv, v, w_proj, b_proj):
    qf = f64(q_feat)
    nrm = np.sqrt((qf * qf).sum(axis=2, keepdims=True))
    q2 = qf / np.maximum(nrm, EPS_NORM)
    t2 = (mxq(q2, 2, "e4m3") @ mxq(f64(kv), 1, "e4m3")) / np.sqrt(N)
    h = f64(v) + t2
    return (mxq(h, 2, "e4m3") @ mxq(f64(w_proj), 0, "e4m3")) + f64(b_proj)

@@ -1,0 +1,301 @@
+import math
+from contextlib import ExitStack
+
+import concourse.mybir as mybir
+from concourse.masks import make_identity
+
+BF16 = mybir.dt.bfloat16
+F32 = mybir.dt.float32
+U32 = mybir.dt.uint32
+U8 = mybir.dt.uint8
+FP8X4 = mybir.dt.float8_e4m3fn_x4
+ALU = mybir.AluOpType
+ACT = mybir.ActivationFunctionType
+
+BATCH, TOKENS, FEATS, OUT_FEATS = 4, 1024, 1024, 256
+EPS_NORM = 1e-12
+FLOPS = 2 * BATCH * TOKENS * FEATS * FEATS + 2 * BATCH * TOKENS * FEATS * OUT_FEATS
+
+P = 128
+PACK = 4
+PASSES = FEATS // (P * PACK)
+WORD_BLOCKS = FEATS // (2 * P)
+
+TILES = TOKENS // P
+N_TILES = BATCH * TILES
+GROUP = 4
+N_GROUPS = N_TILES // GROUP
+PAIR = 2
+
+PIECE_COLS = 256
+PIECES = PASSES * FEATS // PIECE_COLS
+N_PIECES = BATCH * PIECES
+
+AHEAD_KV_REGROUP = 10
+AHEAD_KV_QUANTISE = 9
+AHEAD_SUM_SQUARES = 8
+AHEAD_NORMALISE = 4
+AHEAD_TRANSPOSE = 3
+AHEAD_QUANTISE_Q2 = 2
+AHEAD_READOUT = 1
+BEHIND_PROJECT = 1
+AHEAD_LOAD = 14
+W_STEP = 0
+FIRST_STEP = -AHEAD_LOAD
+LAST_STEP = N_TILES - 1 + BEHIND_PROJECT
+
+
+def tile_essattn_pb_t_kernel(tc, q_feat, kv, v, w_proj, b_proj, out):
+    nc = tc.nc
+
+    q_rows = q_feat.rearrange("b (p t) f -> b p t f", t=TILES)
+    v_rows = v.rearrange("b (p t) f -> b p t f", t=TILES)
+    out_rows = out.rearrange("b (p t) n -> b p t n", t=TILES)
+    kv_rows = kv.rearrange("b (cu p e) w -> b p cu (e w)", p=P, e=2)
+    w_rows = w_proj.rearrange("(cu p e) n -> p cu (e n)", p=P, e=2)
+
+    with ExitStack() as ctx:
+        const = ctx.enter_context(tc.tile_pool(name="const", bufs=1))
+        q_pool = ctx.enter_context(tc.tile_pool(name="q_nat", bufs=4))
+        v_pool = ctx.enter_context(tc.tile_pool(name="v_nat", bufs=3))
+        kv_pool = ctx.enter_context(tc.tile_pool(name="kv", bufs=2))
+        work = ctx.enter_context(tc.tile_pool(name="work", bufs=3))
+        vt_pool = ctx.enter_context(tc.tile_pool(name="vT", bufs=5))
+        out_pool = ctx.enter_context(tc.tile_pool(name="out", bufs=2))
+        turn_psum = ctx.enter_context(tc.psum_pool(name="turn_psum", bufs=3))
+        t2_psum = ctx.enter_context(tc.psum_pool(name="t2_psum", bufs=4))
+        out_psum = ctx.enter_context(tc.psum_pool(name="out_psum", bufs=1))
+        ctx.enter_context(tc.manual_schedule())
+
+        q_nat, v_nat, kv_raw, kv_grp, kv_codes, kv_scales = {}, {}, {}, {}, {}, {}
+        sumsq, norm, inv_norm = {}, {}, {}
+        q2_nat, q2_grp, q2_codes, q2_scales = {}, {}, {}, {}
+        vT_grp, t2_bank, hT_grp, h_codes, h_scales = {}, {}, {}, {}, {}
+        out_bank, out_sb = {}, {}
+
+        ident = const.tile([P, P], F32, name="ident")
+        make_identity(nc, ident[:])
+
+        one = const.tile([P, 1], F32, name="one")
+        one_root = const.tile([P, 1], F32, name="one_root")
+        nc.vector.memset(one[:], 1.0)
+        nc.scalar.sqrt(one_root[:], one[:])
+
+        w_raw = const.tile([P, PASSES, PACK, OUT_FEATS], BF16, name="w_raw")
+        w_grp = const.tile([P, PASSES, OUT_FEATS, PACK], BF16, name="w_grp", align_bytes=64)
+        w_codes = const.tile([P, PASSES, OUT_FEATS], U32, name="w_codes", align_bytes=64)
+        w_scales = const.tile([P, PASSES, OUT_FEATS], U8, name="w_scales", align_bytes=64)
+        bias = const.tile([P, OUT_FEATS], BF16, name="bias")
+
+        def issue_loads(slot):
+            if 0 <= slot < N_GROUPS:
+                b, first = divmod(slot * GROUP, TILES)
+                q_nat[slot] = q_pool.tile([P, GROUP, FEATS], BF16, name="q_nat")
+                nc.sync.dma_start(out=q_nat[slot][:], in_=q_rows[b, :, first : first + GROUP, :])
+            if 0 <= slot - 1 < N_GROUPS:
+                b, first = divmod((slot - 1) * GROUP, TILES)
+                v_nat[slot - 1] = v_pool.tile([P, GROUP, FEATS], BF16, name="v_nat")
+                nc.sync.dma_start(out=v_nat[slot - 1][:], in_=v_rows[b, :, first : first + GROUP, :])
+            if slot == 1:
+                nc.sync.dma_start(
+                    out=w_raw[:].rearrange("p c (u e) n -> p (c u) (e n)", e=2), in_=w_rows
+                )
+                nc.sync.dma_start(out=bias[:], in_=b_proj.partition_broadcast(P))
+            if slot % 2 == 0 and 0 <= slot // 2 < BATCH:
+                b = slot // 2
+                kv_raw[b] = kv_pool.tile([P, PASSES, PACK, FEATS], BF16, name="kv_raw")
+                nc.sync.dma_start(
+                    out=kv_raw[b][:].rearrange("p c (u e) w -> p (c u) (e w)", e=2), in_=kv_rows[b]
+                )
+
+        def regroup_kv(k):
+            if not 0 <= k < N_PIECES:
+                return
+            b, c, a = k // PIECES, (k % PIECES) // 4, k % 4
+            kv_grp[k] = work.tile([P, 2, P, PACK], BF16, name="kv_grp", align_bytes=64)
+            source = kv_raw[b][:, c, :, a * PIECE_COLS : (a + 1) * PIECE_COLS]
+            copy = nc.vector.tensor_copy if k % 2 == 0 else nc.scalar.copy
+            copy(
+                out=kv_grp[k][:].rearrange("p e m t -> p m t e"),
+                in_=source.rearrange("p t (m e) -> p m t e", e=2),
+            )
+
+        def quantise_kv(k):
+            if not 0 <= k < N_PIECES:
+                return
+            b, c, a = k // PIECES, (k % PIECES) // 4, k % 4
+            if k % PIECES == 0:
+                kv_codes[b] = kv_pool.tile([P, PASSES, FEATS], U32, name="kv_codes", align_bytes=64)
+                kv_scales[b] = kv_pool.tile([P, PASSES, FEATS], U8, name="kv_scales", align_bytes=64)
+            cols = slice(a * PIECE_COLS, (a + 1) * PIECE_COLS)
+            nc.vector.quantize_mx(
+                out=kv_codes[b][:, c, cols].bitcast(FP8X4),
+                scales=kv_scales[b][:, c, cols],
+                in_=kv_grp[k][:].rearrange("p e m t -> p (e m t)"),
+            )
+
+        def regroup_w():
+            nc.vector.tensor_copy(out=w_grp[:], in_=w_raw[:].rearrange("p c t n -> p c n t"))
+
+        def quantise_w():
+            nc.vector.quantize_mx(
+                out=w_codes[:].rearrange("p c n -> p (c n)").bitcast(FP8X4),
+                scales=w_scales[:].rearrange("p c n -> p (c n)"),
+                in_=w_grp[:].rearrange("p c n t -> p (c n t)"),
+            )
+
+        def sum_squares(n):
+            if not 0 <= n < N_TILES:
+                return
+            g, i = divmod(n, GROUP)
+            if i == 0:
+                sumsq[g] = work.tile([P, GROUP], F32, name="sumsq")
+            squares = work.tile([P, FEATS], BF16, name="squares")
+            nc.scalar.activation(
+                out=squares[:], in_=q_nat[g][:, i, :], func=ACT.Square, accum_out=sumsq[g][:, i : i + 1]
+            )
+            if i == GROUP - 1:
+                norm[g] = work.tile([P, GROUP], F32, name="norm")
+                nc.scalar.sqrt(norm[g][:], sumsq[g][:])
+
+        def invert_norms(n):
+            if not 0 <= n < N_TILES or n % GROUP != GROUP - 1:
+                return
+            g = n // GROUP
+            floored = work.tile([P, GROUP], F32, name="floored")
+            inv_norm[g] = work.tile([P, GROUP], F32, name="inv_norm")
+            nc.vector.tensor_scalar_max(out=floored[:], in0=norm[g][:], scalar1=EPS_NORM)
+            nc.vector.reciprocal(out=inv_norm[g][:], in_=floored[:])
+
+        def normalise(n):
+            if not 0 <= n < N_TILES:
+                return
+            g, i = divmod(n, GROUP)
+            q2_nat[n] = work.tile([P, FEATS], BF16, name="q2_nat")
+            nc.vector.tensor_scalar_mul(
+                out=q2_nat[n][:], in0=q_nat[g][:, i, :], scalar1=inv_norm[g][:, i : i + 1]
+            )
+
+        def turn(natural, pool, name):
+            words = natural.bitcast(F32)
+            bank = turn_psum.tile([P, WORD_BLOCKS, P], F32, name="turn_bank")
+            for block in range(WORD_BLOCKS):
+                nc.tensor.transpose(
+                    out=bank[:, block, :], in_=words[:, block * P : (block + 1) * P], identity=ident[:]
+                )
+            grouped = pool.tile([P, PASSES, P, PACK], BF16, name=name, align_bytes=64)
+            nc.scalar.copy(
+                out=grouped[:].bitcast(F32), in_=bank[:].rearrange("p (c u) k -> p c k u", u=2)
+            )
+            return grouped
+
+        def transpose_q2_and_v(n):
+            if not 0 <= n < N_TILES:
+                return
+            g, i = divmod(n, GROUP)
+            q2_grp[n] = turn(q2_nat[n][:], work, "q2_grp")
+            vT_grp[n] = turn(v_nat[g][:, i, :], vt_pool, "vT_grp")
+
+        def quantise_tile(grouped, name):
+            codes = work.tile([P, PASSES, P], U32, name=name + "_codes", align_bytes=64)
+            scales = work.tile([P, PASSES, P], U8, name=name + "_scales", align_bytes=64)
+            nc.vector.quantize_mx(
+                out=codes[:].rearrange("p c k -> p (c k)").bitcast(FP8X4),
+                scales=scales[:].rearrange("p c k -> p (c k)"),
+                in_=grouped[:].rearrange("p c k t -> p (c k t)"),
+            )
+            return codes, scales
+
+        def quantise_q2(n):
+            if 0 <= n < N_TILES:
+                q2_codes[n], q2_scales[n] = quantise_tile(q2_grp[n], "q2")
+
+        def readout(n):
+            if not 0 <= n < N_TILES:
+                return
+            b = n // TILES
+            for c2 in range(PASSES):
+                t2_bank[n, c2] = t2_psum.tile([P, PACK, P], F32, name="t2_bank")
+                for t in range(PACK):
+                    cols = slice((c2 * PACK + t) * P, (c2 * PACK + t + 1) * P)
+                    for c in range(PASSES):
+                        nc.tensor.matmul_mx(
+                            out=t2_bank[n, c2][:, t, :],
+                            lhsT=kv_codes[b][:, c, cols].bitcast(FP8X4),
+                            lhsT_scale=kv_scales[b][:, c, cols],
+                            rhs=q2_codes[n][:, c, :].bitcast(FP8X4),
+                            rhs_scale=q2_scales[n][:, c, :],
+                            start=(c == 0),
+                            stop=(c == PASSES - 1),
+                        )
+
+        def add_values(n):
+            if not 0 <= n < N_TILES:
+                return
+            hT_grp[n] = work.tile([P, PASSES, P, PACK], BF16, name="hT_grp", align_bytes=64)
+            for c2 in range(PASSES):
+                nc.vector.scalar_tensor_tensor(
+                    out=hT_grp[n][:, c2],
+                    in0=t2_bank[n, c2][:].rearrange("p t k -> p k t"),
+                    scalar=1.0 / math.sqrt(TOKENS),
+                    in1=vT_grp[n][:, c2],
+                    op0=ALU.mult,
+                    op1=ALU.add,
+                )
+
+        def quantise_h(n):
+            if 0 <= n < N_TILES:
+                h_codes[n], h_scales[n] = quantise_tile(hT_grp[n], "h")
+
+        def project(n):
+            if not 0 <= n < N_TILES:
+                return
+            pair, half = divmod(n, PAIR)
+            if half == 0:
+                out_bank[pair] = out_psum.tile([P, PAIR, OUT_FEATS], F32, name="out_bank")
+            for c2 in range(PASSES):
+                nc.tensor.matmul_mx(
+                    out=out_bank[pair][:, half, :],
+                    lhsT=h_codes[n][:, c2, :].bitcast(FP8X4),
+                    lhsT_scale=h_scales[n][:, c2, :],
+                    rhs=w_codes[:, c2, :].bitcast(FP8X4),
+                    rhs_scale=w_scales[:, c2, :],
+                    start=(c2 == 0),
+                    stop=(c2 == PASSES - 1),
+                )
+
+        def add_bias_and_store(n):
+            if not 0 <= n < N_TILES or n % PAIR != PAIR - 1:
+                return
+            g, i = divmod(n, GROUP)
+            if i == PAIR - 1:
+                out_sb[g] = out_pool.tile([P, GROUP, OUT_FEATS], F32, name="out_sb")
+            nc.vector.tensor_tensor(
+                out=out_sb[g][:, i - 1 : i + 1, :],
+                in0=out_bank[n // PAIR][:],
+                in1=bias[:].unsqueeze(1).to_broadcast([P, PAIR, OUT_FEATS]),
+                op=ALU.add,
+            )
+            if i == GROUP - 1:
+                b, first = divmod(g * GROUP, TILES)
+                nc.sync.dma_start(out=out_rows[b, :, first : first + GROUP, :], in_=out_sb[g][:])
+
+        for s in range(FIRST_STEP, LAST_STEP + 1):
+            if (s + AHEAD_LOAD) % GROUP == 0:
+                issue_loads((s + AHEAD_LOAD) // GROUP)
+            project(s - BEHIND_PROJECT)
+            transpose_q2_and_v(s + AHEAD_TRANSPOSE)
+            readout(s + AHEAD_READOUT)
+            add_values(s)
+            sum_squares(s + AHEAD_SUM_SQUARES)
+            normalise(s + AHEAD_NORMALISE)
+            quantise_q2(s + AHEAD_QUANTISE_Q2)
+            quantise_h(s)
+            if s == W_STEP:
+                regroup_w()
+            regroup_kv(s + AHEAD_KV_REGROUP)
+            quantise_kv(s + AHEAD_KV_QUANTISE)
+            if s == W_STEP:
+                quantise_w()
+            add_bias_and_store(s - BEHIND_PROJECT)
+            invert_norms(s + AHEAD_SUM_SQUARES)

@@ -65,7 +65,6 @@ def tile_essattn_pb_t_kernel(tc, q_feat, kv, v, w_proj, b_proj, out):
         turn_psum = ctx.enter_context(tc.psum_pool(name="turn_psum", bufs=3))
         t2_psum = ctx.enter_context(tc.psum_pool(name="t2_psum", bufs=4))
         out_psum = ctx.enter_context(tc.psum_pool(name="out_psum", bufs=1))
-        ctx.enter_context(tc.manual_schedule())
 
         q_nat, v_nat, kv_raw, kv_grp, kv_codes, kv_scales = {}, {}, {}, {}, {}, {}
         sumsq, norm, inv_norm = {}, {}, {}

@@ -39,9 +39,8 @@ AHEAD_TRANSPOSE = 3
 AHEAD_QUANTISE_Q2 = 2
 AHEAD_READOUT = 1
 BEHIND_PROJECT = 1
-AHEAD_LOAD = 14
+FIRST_STEP = -14
 W_STEP = 0
-FIRST_STEP = -AHEAD_LOAD
 LAST_STEP = N_TILES - 1 + BEHIND_PROJECT
 
 
@@ -51,17 +50,18 @@ def tile_essattn_pb_t_kernel(tc, q_feat, kv, v, w_proj, b_proj, out):
     q_rows = q_feat.rearrange("b (p t) f -> b p t f", t=TILES)
     v_rows = v.rearrange("b (p t) f -> b p t f", t=TILES)
     out_rows = out.rearrange("b (p t) n -> b p t n", t=TILES)
-    kv_rows = kv.rearrange("b (cu p e) w -> b p cu (e w)", p=P, e=2)
+    kv_rows = kv.rearrange("b (c u p e) w -> b c p u (e w)", c=PASSES, p=P, e=2)
     w_rows = w_proj.rearrange("(cu p e) n -> p cu (e n)", p=P, e=2)
 
     with ExitStack() as ctx:
         const = ctx.enter_context(tc.tile_pool(name="const", bufs=1))
         q_pool = ctx.enter_context(tc.tile_pool(name="q_nat", bufs=4))
         v_pool = ctx.enter_context(tc.tile_pool(name="v_nat", bufs=3))
+        kv_raw_pool = ctx.enter_context(tc.tile_pool(name="kv_raw", bufs=3))
         kv_pool = ctx.enter_context(tc.tile_pool(name="kv", bufs=2))
         work = ctx.enter_context(tc.tile_pool(name="work", bufs=3))
         vt_pool = ctx.enter_context(tc.tile_pool(name="vT", bufs=5))
-        out_pool = ctx.enter_context(tc.tile_pool(name="out", bufs=2))
+        out_pool = ctx.enter_context(tc.tile_pool(name="out", bufs=3))
         turn_psum = ctx.enter_context(tc.psum_pool(name="turn_psum", bufs=3))
         t2_psum = ctx.enter_context(tc.psum_pool(name="t2_psum", bufs=4))
         out_psum = ctx.enter_context(tc.psum_pool(name="out_psum", bufs=1))
@@ -70,7 +70,7 @@ def tile_essattn_pb_t_kernel(tc, q_feat, kv, v, w_proj, b_proj, out):
         sumsq, norm, inv_norm = {}, {}, {}
         q2_nat, q2_grp, q2_codes, q2_scales = {}, {}, {}, {}
         vT_grp, t2_bank, hT_grp, h_codes, h_scales = {}, {}, {}, {}, {}
-        out_bank, out_sb = {}, {}
+        out_bank = {}
 
         ident = const.tile([P, P], F32, name="ident")
         make_identity(nc, ident[:])
@@ -86,34 +86,33 @@ def tile_essattn_pb_t_kernel(tc, q_feat, kv, v, w_proj, b_proj, out):
         w_scales = const.tile([P, PASSES, OUT_FEATS], U8, name="w_scales", align_bytes=64)
         bias = const.tile([P, OUT_FEATS], BF16, name="bias")
 
-        def issue_loads(slot):
-            if 0 <= slot < N_GROUPS:
-                b, first = divmod(slot * GROUP, TILES)
-                q_nat[slot] = q_pool.tile([P, GROUP, FEATS], BF16, name="q_nat")
-                nc.sync.dma_start(out=q_nat[slot][:], in_=q_rows[b, :, first : first + GROUP, :])
-            if 0 <= slot - 1 < N_GROUPS:
-                b, first = divmod((slot - 1) * GROUP, TILES)
-                v_nat[slot - 1] = v_pool.tile([P, GROUP, FEATS], BF16, name="v_nat")
-                nc.sync.dma_start(out=v_nat[slot - 1][:], in_=v_rows[b, :, first : first + GROUP, :])
-            if slot == 1:
+        def issue_loads(g):
+            if 0 <= g < N_GROUPS:
+                b, c = divmod(g, PASSES)
+                kv_raw[g] = kv_raw_pool.tile([P, PACK, FEATS], BF16, name="kv_raw")
+                nc.sync.dma_start(
+                    out=kv_raw[g][:].rearrange("p (u e) w -> p u (e w)", e=2), in_=kv_rows[b, c]
+                )
+                b, first = divmod(g * GROUP, TILES)
+                q_nat[g] = q_pool.tile([P, GROUP, FEATS], BF16, name="q_nat")
+                nc.sync.dma_start(out=q_nat[g][:], in_=q_rows[b, :, first : first + GROUP, :])
+            if 0 <= g - 1 < N_GROUPS:
+                b, first = divmod((g - 1) * GROUP, TILES)
+                v_nat[g - 1] = v_pool.tile([P, GROUP, FEATS], BF16, name="v_nat")
+                nc.sync.dma_start(out=v_nat[g - 1][:], in_=v_rows[b, :, first : first + GROUP, :])
+            if g == 1:
                 nc.sync.dma_start(
                     out=w_raw[:].rearrange("p c (u e) n -> p (c u) (e n)", e=2), in_=w_rows
                 )
                 nc.sync.dma_start(out=bias[:], in_=b_proj.partition_broadcast(P))
-            if slot % 2 == 0 and 0 <= slot // 2 < BATCH:
-                b = slot // 2
-                kv_raw[b] = kv_pool.tile([P, PASSES, PACK, FEATS], BF16, name="kv_raw")
-                nc.sync.dma_start(
-                    out=kv_raw[b][:].rearrange("p c (u e) w -> p (c u) (e w)", e=2), in_=kv_rows[b]
-                )
 
         def regroup_kv(k):
             if not 0 <= k < N_PIECES:
                 return
-            b, c, a = k // PIECES, (k % PIECES) // 4, k % 4
+            half, a = divmod(k, PIECES // PASSES)
             kv_grp[k] = work.tile([P, 2, P, PACK], BF16, name="kv_grp", align_bytes=64)
-            source = kv_raw[b][:, c, :, a * PIECE_COLS : (a + 1) * PIECE_COLS]
-            copy = nc.vector.tensor_copy if k % 2 == 0 else nc.scalar.copy
+            source = kv_raw[half][:, :, a * PIECE_COLS : (a + 1) * PIECE_COLS]
+            copy = nc.vector.tensor_copy if k % 2 == 0 or k < PIECES else nc.scalar.copy
             copy(
                 out=kv_grp[k][:].rearrange("p e m t -> p m t e"),
                 in_=source.rearrange("p t (m e) -> p m t e", e=2),
@@ -266,22 +265,19 @@ def tile_essattn_pb_t_kernel(tc, q_feat, kv, v, w_proj, b_proj, out):
         def add_bias_and_store(n):
             if not 0 <= n < N_TILES or n % PAIR != PAIR - 1:
                 return
-            g, i = divmod(n, GROUP)
-            if i == PAIR - 1:
-                out_sb[g] = out_pool.tile([P, GROUP, OUT_FEATS], F32, name="out_sb")
+            out_sb = out_pool.tile([P, PAIR, OUT_FEATS], F32, name="out_sb")
             nc.vector.tensor_tensor(
-                out=out_sb[g][:, i - 1 : i + 1, :],
+                out=out_sb[:],
                 in0=out_bank[n // PAIR][:],
                 in1=bias[:].unsqueeze(1).to_broadcast([P, PAIR, OUT_FEATS]),
                 op=ALU.add,
             )
-            if i == GROUP - 1:
-                b, first = divmod(g * GROUP, TILES)
-                nc.sync.dma_start(out=out_rows[b, :, first : first + GROUP, :], in_=out_sb[g][:])
+            b, last = divmod(n, TILES)
+            nc.sync.dma_start(out=out_rows[b, :, last + 1 - PAIR : last + 1, :], in_=out_sb[:])
 
         for s in range(FIRST_STEP, LAST_STEP + 1):
-            if (s + AHEAD_LOAD) % GROUP == 0:
-                issue_loads((s + AHEAD_LOAD) // GROUP)
+            if (s - FIRST_STEP) % GROUP == 0:
+                issue_loads((s - FIRST_STEP) // GROUP)
             project(s - BEHIND_PROJECT)
             transpose_q2_and_v(s + AHEAD_TRANSPOSE)
             readout(s + AHEAD_READOUT)

@@ -20,6 +20,8 @@ P = 128
 PACK = 4
 PASSES = FEATS // (P * PACK)
 WORD_BLOCKS = FEATS // (2 * P)
+BANK_COLS = 512
+HALVES = FEATS // BANK_COLS
 
 TILES = TOKENS // P
 N_TILES = BATCH * TILES
@@ -28,6 +30,7 @@ N_GROUPS = N_TILES // GROUP
 PAIR = 2
 
 PIECE_COLS = 256
+RUN = 4
 PIECES = PASSES * FEATS // PIECE_COLS
 N_PIECES = BATCH * PIECES
 
@@ -38,7 +41,9 @@ AHEAD_NORMALISE = 4
 AHEAD_TRANSPOSE = 3
 AHEAD_QUANTISE_Q2 = 2
 AHEAD_READOUT = 1
-BEHIND_PROJECT = 1
+BEHIND_TRANSPOSE = 1
+BEHIND_QUANTISE_H = 2
+BEHIND_PROJECT = 3
 FIRST_STEP = -14
 W_STEP = 0
 LAST_STEP = N_TILES - 1 + BEHIND_PROJECT
@@ -60,7 +65,6 @@ def tile_essattn_pb_t_kernel(tc, q_feat, kv, v, w_proj, b_proj, out):
         kv_raw_pool = ctx.enter_context(tc.tile_pool(name="kv_raw", bufs=3))
         kv_pool = ctx.enter_context(tc.tile_pool(name="kv", bufs=2))
         work = ctx.enter_context(tc.tile_pool(name="work", bufs=3))
-        vt_pool = ctx.enter_context(tc.tile_pool(name="vT", bufs=5))
         out_pool = ctx.enter_context(tc.tile_pool(name="out", bufs=3))
         turn_psum = ctx.enter_context(tc.psum_pool(name="turn_psum", bufs=3))
         t2_psum = ctx.enter_context(tc.psum_pool(name="t2_psum", bufs=4))
@@ -69,7 +73,7 @@ def tile_essattn_pb_t_kernel(tc, q_feat, kv, v, w_proj, b_proj, out):
         q_nat, v_nat, kv_raw, kv_grp, kv_codes, kv_scales = {}, {}, {}, {}, {}, {}
         sumsq, norm, inv_norm = {}, {}, {}
         q2_nat, q2_grp, q2_codes, q2_scales = {}, {}, {}, {}
-        vT_grp, t2_bank, hT_grp, h_codes, h_scales = {}, {}, {}, {}, {}
+        t2_bank, h_nat, hT_grp, h_codes, h_scales = {}, {}, {}, {}, {}
         out_bank = {}
 
         ident = const.tile([P, P], F32, name="ident")
@@ -110,12 +114,12 @@ def tile_essattn_pb_t_kernel(tc, q_feat, kv, v, w_proj, b_proj, out):
             if not 0 <= k < N_PIECES:
                 return
             half, a = divmod(k, PIECES // PASSES)
-            kv_grp[k] = work.tile([P, 2, P, PACK], BF16, name="kv_grp", align_bytes=64)
+            kv_grp[k] = work.tile([P, PIECE_COLS, PACK], BF16, name="kv_grp", align_bytes=64)
             source = kv_raw[half][:, :, a * PIECE_COLS : (a + 1) * PIECE_COLS]
             copy = nc.vector.tensor_copy if k % 2 == 0 or k < PIECES else nc.scalar.copy
             copy(
-                out=kv_grp[k][:].rearrange("p e m t -> p m t e"),
-                in_=source.rearrange("p t (m e) -> p m t e", e=2),
+                out=kv_grp[k][:].rearrange("p (c i) t -> p c t i", i=RUN),
+                in_=source.rearrange("p t (c i) -> p c t i", i=RUN),
             )
 
         def quantise_kv(k):
@@ -129,7 +133,7 @@ def tile_essattn_pb_t_kernel(tc, q_feat, kv, v, w_proj, b_proj, out):
             nc.vector.quantize_mx(
                 out=kv_codes[b][:, c, cols].bitcast(FP8X4),
                 scales=kv_scales[b][:, c, cols],
-                in_=kv_grp[k][:].rearrange("p e m t -> p (e m t)"),
+                in_=kv_grp[k][:].rearrange("p m t -> p (m t)"),
             )
 
         def regroup_w():
@@ -174,25 +178,26 @@ def tile_essattn_pb_t_kernel(tc, q_feat, kv, v, w_proj, b_proj, out):
                 out=q2_nat[n][:], in0=q_nat[g][:, i, :], scalar1=inv_norm[g][:, i : i + 1]
             )
 
-        def turn(natural, pool, name):
+        def turn(natural, name):
             words = natural.bitcast(F32)
             bank = turn_psum.tile([P, WORD_BLOCKS, P], F32, name="turn_bank")
             for block in range(WORD_BLOCKS):
                 nc.tensor.transpose(
                     out=bank[:, block, :], in_=words[:, block * P : (block + 1) * P], identity=ident[:]
                 )
-            grouped = pool.tile([P, PASSES, P, PACK], BF16, name=name, align_bytes=64)
+            grouped = work.tile([P, PASSES, P, PACK], BF16, name=name, align_bytes=64)
             nc.scalar.copy(
                 out=grouped[:].bitcast(F32), in_=bank[:].rearrange("p (c u) k -> p c k u", u=2)
             )
             return grouped
 
-        def transpose_q2_and_v(n):
-            if not 0 <= n < N_TILES:
-                return
-            g, i = divmod(n, GROUP)
-            q2_grp[n] = turn(q2_nat[n][:], work, "q2_grp")
-            vT_grp[n] = turn(v_nat[g][:, i, :], vt_pool, "vT_grp")
+        def transpose_q2(n):
+            if 0 <= n < N_TILES:
+                q2_grp[n] = turn(q2_nat[n][:], "q2_grp")
+
+        def transpose_h(n):
+            if 0 <= n < N_TILES:
+                hT_grp[n] = turn(h_nat[n][:], "hT_grp")
 
         def quantise_tile(grouped, name):
             codes = work.tile([P, PASSES, P], U32, name=name + "_codes", align_bytes=64)
@@ -212,31 +217,32 @@ def tile_essattn_pb_t_kernel(tc, q_feat, kv, v, w_proj, b_proj, out):
             if not 0 <= n < N_TILES:
                 return
             b = n // TILES
-            for c2 in range(PASSES):
-                t2_bank[n, c2] = t2_psum.tile([P, PACK, P], F32, name="t2_bank")
-                for t in range(PACK):
-                    cols = slice((c2 * PACK + t) * P, (c2 * PACK + t + 1) * P)
-                    for c in range(PASSES):
-                        nc.tensor.matmul_mx(
-                            out=t2_bank[n, c2][:, t, :],
-                            lhsT=kv_codes[b][:, c, cols].bitcast(FP8X4),
-                            lhsT_scale=kv_scales[b][:, c, cols],
-                            rhs=q2_codes[n][:, c, :].bitcast(FP8X4),
-                            rhs_scale=q2_scales[n][:, c, :],
-                            start=(c == 0),
-                            stop=(c == PASSES - 1),
-                        )
+            for half in range(HALVES):
+                t2_bank[n, half] = t2_psum.tile([P, BANK_COLS], F32, name="t2_bank")
+                cols = slice(half * BANK_COLS, (half + 1) * BANK_COLS)
+                for c in range(PASSES):
+                    nc.tensor.matmul_mx(
+                        out=t2_bank[n, half][:],
+                        lhsT=q2_codes[n][:, c, :].bitcast(FP8X4),
+                        lhsT_scale=q2_scales[n][:, c, :],
+                        rhs=kv_codes[b][:, c, cols].bitcast(FP8X4),
+                        rhs_scale=kv_scales[b][:, c, cols],
+                        start=(c == 0),
+                        stop=(c == PASSES - 1),
+                    )
 
         def add_values(n):
             if not 0 <= n < N_TILES:
                 return
-            hT_grp[n] = work.tile([P, PASSES, P, PACK], BF16, name="hT_grp", align_bytes=64)
-            for c2 in range(PASSES):
+            g, i = divmod(n, GROUP)
+            h_nat[n] = work.tile([P, FEATS], BF16, name="h_nat")
+            for half in range(HALVES):
+                cols = slice(half * BANK_COLS, (half + 1) * BANK_COLS)
                 nc.vector.scalar_tensor_tensor(
-                    out=hT_grp[n][:, c2],
-                    in0=t2_bank[n, c2][:].rearrange("p t k -> p k t"),
+                    out=h_nat[n][:, cols],
+                    in0=t2_bank[n, half][:],
                     scalar=1.0 / math.sqrt(TOKENS),
-                    in1=vT_grp[n][:, c2],
+                    in1=v_nat[g][:, i, cols],
                     op0=ALU.mult,
                     op1=ALU.add,
                 )
@@ -279,13 +285,14 @@ def tile_essattn_pb_t_kernel(tc, q_feat, kv, v, w_proj, b_proj, out):
             if (s - FIRST_STEP) % GROUP == 0:
                 issue_loads((s - FIRST_STEP) // GROUP)
             project(s - BEHIND_PROJECT)
-            transpose_q2_and_v(s + AHEAD_TRANSPOSE)
             readout(s + AHEAD_READOUT)
+            transpose_q2(s + AHEAD_TRANSPOSE)
+            transpose_h(s - BEHIND_TRANSPOSE)
             add_values(s)
             sum_squares(s + AHEAD_SUM_SQUARES)
             normalise(s + AHEAD_NORMALISE)
             quantise_q2(s + AHEAD_QUANTISE_Q2)
-            quantise_h(s)
+            quantise_h(s - BEHIND_QUANTISE_H)
             if s == W_STEP:
                 regroup_w()
             regroup_kv(s + AHEAD_KV_REGROUP)

@@ -116,11 +116,20 @@ def tile_essattn_pb_t_kernel(tc, q_feat, kv, v, w_proj, b_proj, out):
             half, a = divmod(k, PIECES // PASSES)
             kv_grp[k] = work.tile([P, PIECE_COLS, PACK], BF16, name="kv_grp", align_bytes=64)
             source = kv_raw[half][:, :, a * PIECE_COLS : (a + 1) * PIECE_COLS]
-            copy = nc.vector.tensor_copy if k % 2 == 0 or k < PIECES else nc.scalar.copy
-            copy(
-                out=kv_grp[k][:].rearrange("p (c i) t -> p c t i", i=RUN),
-                in_=source.rearrange("p t (c i) -> p c t i", i=RUN),
-            )
+            if k < PIECES:
+                nc.vector.tensor_copy(
+                    out=kv_grp[k][:].rearrange("p (c i) t -> p c t i", i=RUN),
+                    in_=source.rearrange("p t (c i) -> p c t i", i=RUN),
+                )
+            else:
+                nc.gpsimd.tensor_scalar(
+                    out=kv_grp[k][:].rearrange("p (c i) t -> p c t i", i=RUN),
+                    in0=source.rearrange("p t (c i) -> p c t i", i=RUN),
+                    scalar1=1.0,
+                    scalar2=0.0,
+                    op0=ALU.mult,
+                    op1=ALU.add,
+                )
 
         def quantise_kv(k):
             if not 0 <= k < N_PIECES:

@@ -33,6 +33,7 @@ PIECE_COLS = 256
 RUN = 4
 PIECES = PASSES * FEATS // PIECE_COLS
 N_PIECES = BATCH * PIECES
+SCALAR_PIECES = (1, 2, 7)
 
 AHEAD_KV_REGROUP = 10
 AHEAD_KV_QUANTISE = 9
@@ -44,9 +45,11 @@ AHEAD_READOUT = 1
 BEHIND_TRANSPOSE = 1
 BEHIND_QUANTISE_H = 2
 BEHIND_PROJECT = 3
-FIRST_STEP = -14
+AHEAD_LOADS = 4
+FIRST_STEP = -AHEAD_KV_REGROUP
 W_STEP = 0
 LAST_STEP = N_TILES - 1 + BEHIND_PROJECT
+NORM_SETS = [(0, 2), (2, 4)] + [(n, n + GROUP) for n in range(GROUP, N_TILES, GROUP)]
 
 
 def tile_essattn_pb_t_kernel(tc, q_feat, kv, v, w_proj, b_proj, out):
@@ -56,13 +59,15 @@ def tile_essattn_pb_t_kernel(tc, q_feat, kv, v, w_proj, b_proj, out):
     v_rows = v.rearrange("b (p t) f -> b p t f", t=TILES)
     out_rows = out.rearrange("b (p t) n -> b p t n", t=TILES)
     kv_rows = kv.rearrange("b (c u p e) w -> b c p u (e w)", c=PASSES, p=P, e=2)
+    kv_part_rows = kv.rearrange("b (c u p e) w -> b c p u e w", c=PASSES, p=P, e=2)
     w_rows = w_proj.rearrange("(cu p e) n -> p cu (e n)", p=P, e=2)
 
     with ExitStack() as ctx:
         const = ctx.enter_context(tc.tile_pool(name="const", bufs=1))
         q_pool = ctx.enter_context(tc.tile_pool(name="q_nat", bufs=4))
-        v_pool = ctx.enter_context(tc.tile_pool(name="v_nat", bufs=3))
-        kv_raw_pool = ctx.enter_context(tc.tile_pool(name="kv_raw", bufs=3))
+        v_pool = ctx.enter_context(tc.tile_pool(name="v_nat", bufs=4))
+        kv_raw_pool = ctx.enter_context(tc.tile_pool(name="kv_raw", bufs=4))
+        piece_pool = ctx.enter_context(tc.tile_pool(name="kv_piece", bufs=1))
         kv_pool = ctx.enter_context(tc.tile_pool(name="kv", bufs=2))
         work = ctx.enter_context(tc.tile_pool(name="work", bufs=3))
         out_pool = ctx.enter_context(tc.tile_pool(name="out", bufs=3))
@@ -72,9 +77,10 @@ def tile_essattn_pb_t_kernel(tc, q_feat, kv, v, w_proj, b_proj, out):
 
         q_nat, v_nat, kv_raw, kv_grp, kv_codes, kv_scales = {}, {}, {}, {}, {}, {}
         sumsq, norm, inv_norm = {}, {}, {}
-        q2_nat, q2_grp, q2_codes, q2_scales = {}, {}, {}, {}
-        t2_bank, h_nat, hT_grp, h_codes, h_scales = {}, {}, {}, {}, {}
+        q2_nat, q2_bank, q2_grp, q2_codes, q2_scales = {}, {}, {}, {}, {}
+        t2_bank, h_nat, h_bank, hT_grp, h_codes, h_scales = {}, {}, {}, {}, {}, {}
         out_bank = {}
+        set_of = {n: (first, end) for first, end in NORM_SETS for n in range(first, end)}
 
         ident = const.tile([P, P], F32, name="ident")
         make_identity(nc, ident[:])
@@ -90,41 +96,69 @@ def tile_essattn_pb_t_kernel(tc, q_feat, kv, v, w_proj, b_proj, out):
         w_scales = const.tile([P, PASSES, OUT_FEATS], U8, name="w_scales", align_bytes=64)
         bias = const.tile([P, OUT_FEATS], BF16, name="bias")
 
-        def issue_loads(g):
-            if 0 <= g < N_GROUPS:
-                b, c = divmod(g, PASSES)
-                kv_raw[g] = kv_raw_pool.tile([P, PACK, FEATS], BF16, name="kv_raw")
+        def load_kv(half, parts=1):
+            b, c = divmod(half, PASSES)
+            kv_raw[half] = kv_raw_pool.tile([P, PACK, FEATS], BF16, name="kv_raw")
+            if parts == 1:
                 nc.sync.dma_start(
-                    out=kv_raw[g][:].rearrange("p (u e) w -> p u (e w)", e=2), in_=kv_rows[b, c]
+                    out=kv_raw[half][:].rearrange("p (u e) w -> p u (e w)", e=2), in_=kv_rows[b, c]
                 )
-                b, first = divmod(g * GROUP, TILES)
-                q_nat[g] = q_pool.tile([P, GROUP, FEATS], BF16, name="q_nat")
-                nc.sync.dma_start(out=q_nat[g][:], in_=q_rows[b, :, first : first + GROUP, :])
-            if 0 <= g - 1 < N_GROUPS:
-                b, first = divmod((g - 1) * GROUP, TILES)
-                v_nat[g - 1] = v_pool.tile([P, GROUP, FEATS], BF16, name="v_nat")
-                nc.sync.dma_start(out=v_nat[g - 1][:], in_=v_rows[b, :, first : first + GROUP, :])
-            if g == 1:
-                nc.sync.dma_start(
-                    out=w_raw[:].rearrange("p c (u e) n -> p (c u) (e n)", e=2), in_=w_rows
-                )
-                nc.sync.dma_start(out=bias[:], in_=b_proj.partition_broadcast(P))
+                return
+            width = FEATS // parts
+            for part in range(parts):
+                cols = slice(part * width, (part + 1) * width)
+                for u in range(2):
+                    nc.sync.dma_start(
+                        out=kv_raw[half][:, 2 * u : 2 * u + 2, cols],
+                        in_=kv_part_rows[b, c, :, u, :, cols],
+                    )
+
+        def load_tokens(tiles, pool, rows, g, name, first=0, count=GROUP):
+            b, start = divmod(g * GROUP, TILES)
+            if g not in tiles:
+                tiles[g] = pool.tile([P, GROUP, FEATS], BF16, name=name)
+            nc.sync.dma_start(
+                out=tiles[g][:, first : first + count, :],
+                in_=rows[b, :, start + first : start + first + count, :],
+            )
+
+        def first_loads():
+            load_kv(0, parts=2)
+            load_tokens(q_nat, q_pool, q_rows, 0, "q_nat", 0, PAIR)
+            load_kv(1, parts=2)
+            load_tokens(q_nat, q_pool, q_rows, 0, "q_nat", PAIR, PAIR)
+            load_tokens(v_nat, v_pool, v_rows, 0, "v_nat")
+            load_tokens(q_nat, q_pool, q_rows, 1, "q_nat")
+            nc.sync.dma_start(
+                out=w_raw[:].rearrange("p c (u e) n -> p (c u) (e n)", e=2), in_=w_rows
+            )
+            nc.sync.dma_start(out=bias[:], in_=b_proj.partition_broadcast(P))
+
+        def later_loads(g):
+            if not 2 <= g <= N_GROUPS:
+                return
+            if g < N_GROUPS:
+                load_kv(g)
+                load_tokens(q_nat, q_pool, q_rows, g, "q_nat")
+            load_tokens(v_nat, v_pool, v_rows, g - 1, "v_nat")
 
         def regroup_kv(k):
             if not 0 <= k < N_PIECES:
                 return
             half, a = divmod(k, PIECES // PASSES)
-            kv_grp[k] = work.tile([P, PIECE_COLS, PACK], BF16, name="kv_grp", align_bytes=64)
             source = kv_raw[half][:, :, a * PIECE_COLS : (a + 1) * PIECE_COLS]
             if k < PIECES:
-                nc.vector.tensor_copy(
+                kv_grp[k] = work.tile([P, PIECE_COLS, PACK], BF16, name="kv_grp", align_bytes=64)
+                copy = nc.scalar.copy if k in SCALAR_PIECES else nc.vector.tensor_copy
+                copy(
                     out=kv_grp[k][:].rearrange("p (c i) t -> p c t i", i=RUN),
                     in_=source.rearrange("p t (c i) -> p c t i", i=RUN),
                 )
             else:
+                kv_grp[k] = piece_pool.tile([P, PIECE_COLS, PACK], BF16, name="kv_piece", align_bytes=64)
                 nc.gpsimd.tensor_scalar(
-                    out=kv_grp[k][:].rearrange("p (c i) t -> p c t i", i=RUN),
-                    in0=source.rearrange("p t (c i) -> p c t i", i=RUN),
+                    out=kv_grp[k][:],
+                    in0=source.rearrange("p t m -> p m t"),
                     scalar1=1.0,
                     scalar2=0.0,
                     op0=ALU.mult,
@@ -145,55 +179,67 @@ def tile_essattn_pb_t_kernel(tc, q_feat, kv, v, w_proj, b_proj, out):
                 in_=kv_grp[k][:].rearrange("p m t -> p (m t)"),
             )
 
-        def regroup_w():
-            nc.vector.tensor_copy(out=w_grp[:], in_=w_raw[:].rearrange("p c t n -> p c n t"))
+        def regroup_w(c):
+            if 0 <= c < PASSES:
+                nc.scalar.copy(out=w_grp[:, c], in_=w_raw[:, c].rearrange("p t n -> p n t"))
 
-        def quantise_w():
-            nc.vector.quantize_mx(
-                out=w_codes[:].rearrange("p c n -> p (c n)").bitcast(FP8X4),
-                scales=w_scales[:].rearrange("p c n -> p (c n)"),
-                in_=w_grp[:].rearrange("p c n t -> p (c n t)"),
-            )
+        def quantise_w(c):
+            if 0 <= c < PASSES:
+                nc.vector.quantize_mx(
+                    out=w_codes[:, c, :].bitcast(FP8X4),
+                    scales=w_scales[:, c, :],
+                    in_=w_grp[:, c].rearrange("p n t -> p (n t)"),
+                )
 
         def sum_squares(n):
             if not 0 <= n < N_TILES:
                 return
             g, i = divmod(n, GROUP)
-            if i == 0:
-                sumsq[g] = work.tile([P, GROUP], F32, name="sumsq")
+            first, end = set_of[n]
+            if n == first:
+                sumsq[first] = work.tile([P, end - first], F32, name="sumsq")
             squares = work.tile([P, FEATS], BF16, name="squares")
             nc.scalar.activation(
-                out=squares[:], in_=q_nat[g][:, i, :], func=ACT.Square, accum_out=sumsq[g][:, i : i + 1]
+                out=squares[:],
+                in_=q_nat[g][:, i, :],
+                func=ACT.Square,
+                accum_out=sumsq[first][:, n - first : n - first + 1],
             )
-            if i == GROUP - 1:
-                norm[g] = work.tile([P, GROUP], F32, name="norm")
-                nc.scalar.sqrt(norm[g][:], sumsq[g][:])
+            if n == end - 1:
+                norm[first] = work.tile([P, end - first], F32, name="norm")
+                nc.scalar.sqrt(norm[first][:], sumsq[first][:])
 
         def invert_norms(n):
-            if not 0 <= n < N_TILES or n % GROUP != GROUP - 1:
+            if not 0 <= n < N_TILES or n != set_of[n][1] - 1:
                 return
-            g = n // GROUP
-            floored = work.tile([P, GROUP], F32, name="floored")
-            inv_norm[g] = work.tile([P, GROUP], F32, name="inv_norm")
-            nc.vector.tensor_scalar_max(out=floored[:], in0=norm[g][:], scalar1=EPS_NORM)
-            nc.vector.reciprocal(out=inv_norm[g][:], in_=floored[:])
+            first, end = set_of[n]
+            floored = work.tile([P, end - first], F32, name="floored")
+            inv_norm[first] = work.tile([P, end - first], F32, name="inv_norm")
+            nc.vector.tensor_scalar_max(out=floored[:], in0=norm[first][:], scalar1=EPS_NORM)
+            nc.vector.reciprocal(out=inv_norm[first][:], in_=floored[:])
 
         def normalise(n):
             if not 0 <= n < N_TILES:
                 return
             g, i = divmod(n, GROUP)
+            first = set_of[n][0]
             q2_nat[n] = work.tile([P, FEATS], BF16, name="q2_nat")
             nc.vector.tensor_scalar_mul(
-                out=q2_nat[n][:], in0=q_nat[g][:, i, :], scalar1=inv_norm[g][:, i : i + 1]
+                out=q2_nat[n][:],
+                in0=q_nat[g][:, i, :],
+                scalar1=inv_norm[first][:, n - first : n - first + 1],
             )
 
-        def turn(natural, name):
+        def turn(natural):
             words = natural.bitcast(F32)
             bank = turn_psum.tile([P, WORD_BLOCKS, P], F32, name="turn_bank")
             for block in range(WORD_BLOCKS):
                 nc.tensor.transpose(
                     out=bank[:, block, :], in_=words[:, block * P : (block + 1) * P], identity=ident[:]
                 )
+            return bank
+
+        def copy_turned(bank, name):
             grouped = work.tile([P, PASSES, P, PACK], BF16, name=name, align_bytes=64)
             nc.scalar.copy(
                 out=grouped[:].bitcast(F32), in_=bank[:].rearrange("p (c u) k -> p c k u", u=2)
@@ -202,11 +248,19 @@ def tile_essattn_pb_t_kernel(tc, q_feat, kv, v, w_proj, b_proj, out):
 
         def transpose_q2(n):
             if 0 <= n < N_TILES:
-                q2_grp[n] = turn(q2_nat[n][:], "q2_grp")
+                q2_bank[n] = turn(q2_nat[n][:])
+
+        def copy_q2(n):
+            if 0 <= n < N_TILES:
+                q2_grp[n] = copy_turned(q2_bank[n], "q2_grp")
 
         def transpose_h(n):
             if 0 <= n < N_TILES:
-                hT_grp[n] = turn(h_nat[n][:], "hT_grp")
+                h_bank[n] = turn(h_nat[n][:])
+
+        def copy_h(n):
+            if 0 <= n < N_TILES:
+                hT_grp[n] = copy_turned(h_bank[n], "hT_grp")
 
         def quantise_tile(grouped, name):
             codes = work.tile([P, PASSES, P], U32, name=name + "_codes", align_bytes=64)
@@ -290,23 +344,28 @@ def tile_essattn_pb_t_kernel(tc, q_feat, kv, v, w_proj, b_proj, out):
             b, last = divmod(n, TILES)
             nc.sync.dma_start(out=out_rows[b, :, last + 1 - PAIR : last + 1, :], in_=out_sb[:])
 
+        ctx.enter_context(tc.manual_schedule())
+        first_loads()
         for s in range(FIRST_STEP, LAST_STEP + 1):
-            if (s - FIRST_STEP) % GROUP == 0:
-                issue_loads((s - FIRST_STEP) // GROUP)
+            if s % GROUP == 0:
+                later_loads(s // GROUP + AHEAD_LOADS)
             project(s - BEHIND_PROJECT)
             readout(s + AHEAD_READOUT)
             transpose_q2(s + AHEAD_TRANSPOSE)
             transpose_h(s - BEHIND_TRANSPOSE)
-            add_values(s)
+            if s + AHEAD_KV_REGROUP < PIECES:
+                regroup_kv(s + AHEAD_KV_REGROUP)
             sum_squares(s + AHEAD_SUM_SQUARES)
+            copy_q2(s + AHEAD_TRANSPOSE)
+            copy_h(s - BEHIND_TRANSPOSE)
+            regroup_w(s - W_STEP)
+            quantise_kv(s + AHEAD_KV_QUANTISE)
+            if s + AHEAD_KV_REGROUP >= PIECES:
+                regroup_kv(s + AHEAD_KV_REGROUP)
+            add_values(s)
+            add_bias_and_store(s - BEHIND_PROJECT)
             normalise(s + AHEAD_NORMALISE)
+            quantise_w(s - W_STEP - 1)
             quantise_q2(s + AHEAD_QUANTISE_Q2)
             quantise_h(s - BEHIND_QUANTISE_H)
-            if s == W_STEP:
-                regroup_w()
-            regroup_kv(s + AHEAD_KV_REGROUP)
-            quantise_kv(s + AHEAD_KV_QUANTISE)
-            if s == W_STEP:
-                quantise_w()
-            add_bias_and_store(s - BEHIND_PROJECT)
             invert_norms(s + AHEAD_SUM_SQUARES)

@@ -28,28 +28,13 @@ N_TILES = BATCH * TILES
 GROUP = 4
 N_GROUPS = N_TILES // GROUP
 PAIR = 2
+N_PAIRS = N_TILES // PAIR
+BATCH_PAIRS = TILES // PAIR
 
-PIECE_COLS = 256
+HALF_COLS = FEATS // 2
+KV_PARTS = PASSES * FEATS // HALF_COLS
+PIECE_COLS = HALF_COLS // 2
 RUN = 4
-PIECES = PASSES * FEATS // PIECE_COLS
-N_PIECES = BATCH * PIECES
-SCALAR_PIECES = (1, 2, 7)
-
-AHEAD_KV_REGROUP = 10
-AHEAD_KV_QUANTISE = 9
-AHEAD_SUM_SQUARES = 8
-AHEAD_NORMALISE = 4
-AHEAD_TRANSPOSE = 3
-AHEAD_QUANTISE_Q2 = 2
-AHEAD_READOUT = 1
-BEHIND_TRANSPOSE = 1
-BEHIND_QUANTISE_H = 2
-BEHIND_PROJECT = 3
-AHEAD_LOADS = 4
-FIRST_STEP = -AHEAD_KV_REGROUP
-W_STEP = 0
-LAST_STEP = N_TILES - 1 + BEHIND_PROJECT
-NORM_SETS = [(0, 2), (2, 4)] + [(n, n + GROUP) for n in range(GROUP, N_TILES, GROUP)]
 
 
 def tile_essattn_pb_t_kernel(tc, q_feat, kv, v, w_proj, b_proj, out):
@@ -67,7 +52,8 @@ def tile_essattn_pb_t_kernel(tc, q_feat, kv, v, w_proj, b_proj, out):
         q_pool = ctx.enter_context(tc.tile_pool(name="q_nat", bufs=4))
         v_pool = ctx.enter_context(tc.tile_pool(name="v_nat", bufs=4))
         kv_raw_pool = ctx.enter_context(tc.tile_pool(name="kv_raw", bufs=4))
-        piece_pool = ctx.enter_context(tc.tile_pool(name="kv_piece", bufs=1))
+        part_pool = ctx.enter_context(tc.tile_pool(name="kv_part", bufs=1))
+        first_pool = ctx.enter_context(tc.tile_pool(name="kv_first", bufs=3))
         kv_pool = ctx.enter_context(tc.tile_pool(name="kv", bufs=2))
         work = ctx.enter_context(tc.tile_pool(name="work", bufs=3))
         out_pool = ctx.enter_context(tc.tile_pool(name="out", bufs=3))
@@ -76,11 +62,10 @@ def tile_essattn_pb_t_kernel(tc, q_feat, kv, v, w_proj, b_proj, out):
         out_psum = ctx.enter_context(tc.psum_pool(name="out_psum", bufs=1))
 
         q_nat, v_nat, kv_raw, kv_grp, kv_codes, kv_scales = {}, {}, {}, {}, {}, {}
-        sumsq, norm, inv_norm = {}, {}, {}
+        sumsq, norm, floored, inv_norm = {}, {}, {}, {}
         q2_nat, q2_bank, q2_grp, q2_codes, q2_scales = {}, {}, {}, {}, {}
         t2_bank, h_nat, h_bank, hT_grp, h_codes, h_scales = {}, {}, {}, {}, {}, {}
-        out_bank = {}
-        set_of = {n: (first, end) for first, end in NORM_SETS for n in range(first, end)}
+        out_bank, out_sb = {}, {}
 
         ident = const.tile([P, P], F32, name="ident")
         make_identity(nc, ident[:])
@@ -96,16 +81,17 @@ def tile_essattn_pb_t_kernel(tc, q_feat, kv, v, w_proj, b_proj, out):
         w_scales = const.tile([P, PASSES, OUT_FEATS], U8, name="w_scales", align_bytes=64)
         bias = const.tile([P, OUT_FEATS], BF16, name="bias")
 
-        def load_kv(half, parts=1):
+        def load_kv(half, parts=1, which=(0, 1)):
             b, c = divmod(half, PASSES)
-            kv_raw[half] = kv_raw_pool.tile([P, PACK, FEATS], BF16, name="kv_raw")
+            if half not in kv_raw:
+                kv_raw[half] = kv_raw_pool.tile([P, PACK, FEATS], BF16, name="kv_raw")
             if parts == 1:
                 nc.sync.dma_start(
                     out=kv_raw[half][:].rearrange("p (u e) w -> p u (e w)", e=2), in_=kv_rows[b, c]
                 )
                 return
             width = FEATS // parts
-            for part in range(parts):
+            for part in which:
                 cols = slice(part * width, (part + 1) * width)
                 for u in range(2):
                     nc.sync.dma_start(
@@ -125,54 +111,65 @@ def tile_essattn_pb_t_kernel(tc, q_feat, kv, v, w_proj, b_proj, out):
         def first_loads():
             load_kv(0, parts=2)
             load_tokens(q_nat, q_pool, q_rows, 0, "q_nat", 0, PAIR)
-            load_kv(1, parts=2)
+            load_kv(1, parts=2, which=(0,))
             load_tokens(q_nat, q_pool, q_rows, 0, "q_nat", PAIR, PAIR)
-            load_tokens(v_nat, v_pool, v_rows, 0, "v_nat")
-            load_tokens(q_nat, q_pool, q_rows, 1, "q_nat")
+            load_kv(1, parts=2, which=(1,))
+            load_tokens(v_nat, v_pool, v_rows, 0, "v_nat", 0, PAIR)
+            load_tokens(q_nat, q_pool, q_rows, 1, "q_nat", 0, PAIR)
+            load_kv(2)
+            load_tokens(v_nat, v_pool, v_rows, 0, "v_nat", PAIR, PAIR)
+            load_tokens(q_nat, q_pool, q_rows, 1, "q_nat", PAIR, PAIR)
             nc.sync.dma_start(
                 out=w_raw[:].rearrange("p c (u e) n -> p (c u) (e n)", e=2), in_=w_rows
             )
             nc.sync.dma_start(out=bias[:], in_=b_proj.partition_broadcast(P))
+            load_kv(3)
 
         def later_loads(g):
-            if not 2 <= g <= N_GROUPS:
-                return
             if g < N_GROUPS:
-                load_kv(g)
                 load_tokens(q_nat, q_pool, q_rows, g, "q_nat")
-            load_tokens(v_nat, v_pool, v_rows, g - 1, "v_nat")
+            if g <= N_GROUPS:
+                load_tokens(v_nat, v_pool, v_rows, g - 1, "v_nat")
+            if g + 2 < N_GROUPS:
+                load_kv(g + 2)
 
-        def regroup_kv(k):
-            if not 0 <= k < N_PIECES:
+        def regroup_piece(k, copy, pool):
+            part, i = divmod(k, HALF_COLS // PIECE_COLS)
+            c, a = divmod(k, FEATS // PIECE_COLS)
+            if i == 0:
+                kv_grp[part] = pool.tile([P, HALF_COLS, PACK], BF16, name="kv_part", align_bytes=64)
+            copy(
+                out=kv_grp[part][:, i * PIECE_COLS : (i + 1) * PIECE_COLS, :].rearrange(
+                    "p (c i) t -> p c t i", i=RUN
+                ),
+                in_=kv_raw[c][:, :, a * PIECE_COLS : (a + 1) * PIECE_COLS].rearrange(
+                    "p t (c i) -> p c t i", i=RUN
+                ),
+            )
+
+        def regroup_part(k):
+            if k >= BATCH * KV_PARTS:
                 return
-            half, a = divmod(k, PIECES // PASSES)
-            source = kv_raw[half][:, :, a * PIECE_COLS : (a + 1) * PIECE_COLS]
-            if k < PIECES:
-                kv_grp[k] = work.tile([P, PIECE_COLS, PACK], BF16, name="kv_grp", align_bytes=64)
-                copy = nc.scalar.copy if k in SCALAR_PIECES else nc.vector.tensor_copy
-                copy(
-                    out=kv_grp[k][:].rearrange("p (c i) t -> p c t i", i=RUN),
-                    in_=source.rearrange("p t (c i) -> p c t i", i=RUN),
-                )
-            else:
-                kv_grp[k] = piece_pool.tile([P, PIECE_COLS, PACK], BF16, name="kv_piece", align_bytes=64)
-                nc.gpsimd.tensor_scalar(
-                    out=kv_grp[k][:],
-                    in0=source.rearrange("p t m -> p m t"),
-                    scalar1=1.0,
-                    scalar2=0.0,
-                    op0=ALU.mult,
-                    op1=ALU.add,
-                )
+            half, a = divmod(k, FEATS // HALF_COLS)
+            kv_grp[k] = part_pool.tile([P, HALF_COLS, PACK], BF16, name="kv_part", align_bytes=64)
+            nc.gpsimd.tensor_scalar(
+                out=kv_grp[k][:],
+                in0=kv_raw[half][:, :, a * HALF_COLS : (a + 1) * HALF_COLS].rearrange("p t m -> p m t"),
+                scalar1=1.0,
+                scalar2=0.0,
+                op0=ALU.mult,
+                op1=ALU.add,
+            )
 
         def quantise_kv(k):
-            if not 0 <= k < N_PIECES:
+            if not 0 <= k < BATCH * KV_PARTS:
                 return
-            b, c, a = k // PIECES, (k % PIECES) // 4, k % 4
-            if k % PIECES == 0:
+            b, ca = divmod(k, KV_PARTS)
+            c, a = divmod(ca, FEATS // HALF_COLS)
+            if ca == 0:
                 kv_codes[b] = kv_pool.tile([P, PASSES, FEATS], U32, name="kv_codes", align_bytes=64)
                 kv_scales[b] = kv_pool.tile([P, PASSES, FEATS], U8, name="kv_scales", align_bytes=64)
-            cols = slice(a * PIECE_COLS, (a + 1) * PIECE_COLS)
+            cols = slice(a * HALF_COLS, (a + 1) * HALF_COLS)
             nc.vector.quantize_mx(
                 out=kv_codes[b][:, c, cols].bitcast(FP8X4),
                 scales=kv_scales[b][:, c, cols],
@@ -180,54 +177,55 @@ def tile_essattn_pb_t_kernel(tc, q_feat, kv, v, w_proj, b_proj, out):
             )
 
         def regroup_w(c):
-            if 0 <= c < PASSES:
-                nc.scalar.copy(out=w_grp[:, c], in_=w_raw[:, c].rearrange("p t n -> p n t"))
+            nc.vector.tensor_copy(out=w_grp[:, c], in_=w_raw[:, c].rearrange("p t n -> p n t"))
 
-        def quantise_w(c):
-            if 0 <= c < PASSES:
-                nc.vector.quantize_mx(
-                    out=w_codes[:, c, :].bitcast(FP8X4),
-                    scales=w_scales[:, c, :],
-                    in_=w_grp[:, c].rearrange("p n t -> p (n t)"),
-                )
-
-        def sum_squares(n):
-            if not 0 <= n < N_TILES:
-                return
-            g, i = divmod(n, GROUP)
-            first, end = set_of[n]
-            if n == first:
-                sumsq[first] = work.tile([P, end - first], F32, name="sumsq")
-            squares = work.tile([P, FEATS], BF16, name="squares")
-            nc.scalar.activation(
-                out=squares[:],
-                in_=q_nat[g][:, i, :],
-                func=ACT.Square,
-                accum_out=sumsq[first][:, n - first : n - first + 1],
+        def quantise_w():
+            nc.vector.quantize_mx(
+                out=w_codes[:].rearrange("p c n -> p (c n)").bitcast(FP8X4),
+                scales=w_scales[:].rearrange("p c n -> p (c n)"),
+                in_=w_grp[:].rearrange("p c n t -> p (c n t)"),
             )
-            if n == end - 1:
-                norm[first] = work.tile([P, end - first], F32, name="norm")
-                nc.scalar.sqrt(norm[first][:], sumsq[first][:])
 
-        def invert_norms(n):
-            if not 0 <= n < N_TILES or n != set_of[n][1] - 1:
-                return
-            first, end = set_of[n]
-            floored = work.tile([P, end - first], F32, name="floored")
-            inv_norm[first] = work.tile([P, end - first], F32, name="inv_norm")
-            nc.vector.tensor_scalar_max(out=floored[:], in0=norm[first][:], scalar1=EPS_NORM)
-            nc.vector.reciprocal(out=inv_norm[first][:], in_=floored[:])
+        def pair_tiles(p):
+            return range(p * PAIR, (p + 1) * PAIR) if 0 <= p < N_PAIRS else ()
+
+        def sum_squares(p):
+            for n in pair_tiles(p):
+                g, i = divmod(n, GROUP)
+                if n % PAIR == 0:
+                    sumsq[p] = work.tile([P, PAIR], F32, name="sumsq")
+                squares = work.tile([P, FEATS], BF16, name="squares")
+                nc.scalar.activation(
+                    out=squares[:],
+                    in_=q_nat[g][:, i, :],
+                    func=ACT.Square,
+                    accum_out=sumsq[p][:, n % PAIR : n % PAIR + 1],
+                )
+                if n % PAIR == PAIR - 1:
+                    norm[p] = work.tile([P, PAIR], F32, name="norm")
+                    nc.scalar.sqrt(norm[p][:], sumsq[p][:])
+
+        def floor_norms(p):
+            if 0 <= p < N_PAIRS:
+                floored[p] = work.tile([P, PAIR], F32, name="floored")
+                nc.vector.tensor_scalar_max(out=floored[p][:], in0=norm[p][:], scalar1=EPS_NORM)
+
+        def invert_norms(p):
+            if 0 <= p < N_PAIRS:
+                inv_norm[p] = work.tile([P, PAIR], F32, name="inv_norm")
+                nc.vector.reciprocal(out=inv_norm[p][:], in_=floored[p][:])
 
         def normalise(n):
             if not 0 <= n < N_TILES:
                 return
             g, i = divmod(n, GROUP)
-            first = set_of[n][0]
-            q2_nat[n] = work.tile([P, FEATS], BF16, name="q2_nat")
+            p, half = divmod(n, PAIR)
+            if half == 0:
+                q2_nat[p] = work.tile([P, PAIR, FEATS], BF16, name="q2_nat")
             nc.vector.tensor_scalar_mul(
-                out=q2_nat[n][:],
+                out=q2_nat[p][:, half, :],
                 in0=q_nat[g][:, i, :],
-                scalar1=inv_norm[first][:, n - first : n - first + 1],
+                scalar1=inv_norm[p][:, half : half + 1],
             )
 
         def turn(natural):
@@ -239,133 +237,223 @@ def tile_essattn_pb_t_kernel(tc, q_feat, kv, v, w_proj, b_proj, out):
                 )
             return bank
 
-        def copy_turned(bank, name):
-            grouped = work.tile([P, PASSES, P, PACK], BF16, name=name, align_bytes=64)
+        def copy_turned(bank, grouped):
             nc.scalar.copy(
-                out=grouped[:].bitcast(F32), in_=bank[:].rearrange("p (c u) k -> p c k u", u=2)
+                out=grouped.bitcast(F32), in_=bank[:].rearrange("p (c u) k -> p c k u", u=2)
             )
-            return grouped
 
-        def transpose_q2(n):
-            if 0 <= n < N_TILES:
-                q2_bank[n] = turn(q2_nat[n][:])
+        def transpose_q2(p):
+            for n in pair_tiles(p):
+                q2_bank[n] = turn(q2_nat[p][:, n % PAIR, :])
 
-        def copy_q2(n):
-            if 0 <= n < N_TILES:
-                q2_grp[n] = copy_turned(q2_bank[n], "q2_grp")
+        def copy_q2(p):
+            if 0 <= p < N_PAIRS:
+                q2_grp[p] = work.tile([P, PAIR, PASSES, P, PACK], BF16, name="q2_grp", align_bytes=64)
+            for n in pair_tiles(p):
+                copy_turned(q2_bank[n], q2_grp[p][:, n % PAIR])
 
         def transpose_h(n):
-            if 0 <= n < N_TILES:
-                h_bank[n] = turn(h_nat[n][:])
+            h_bank[n] = turn(h_nat[n // PAIR][:, n % PAIR, :])
 
         def copy_h(n):
-            if 0 <= n < N_TILES:
-                hT_grp[n] = copy_turned(h_bank[n], "hT_grp")
+            p, half = divmod(n, PAIR)
+            if half == 0:
+                hT_grp[p] = work.tile([P, PAIR, PASSES, P, PACK], BF16, name="hT_grp", align_bytes=64)
+            copy_turned(h_bank[n], hT_grp[p][:, half])
 
-        def quantise_tile(grouped, name):
-            codes = work.tile([P, PASSES, P], U32, name=name + "_codes", align_bytes=64)
-            scales = work.tile([P, PASSES, P], U8, name=name + "_scales", align_bytes=64)
-            nc.vector.quantize_mx(
-                out=codes[:].rearrange("p c k -> p (c k)").bitcast(FP8X4),
-                scales=scales[:].rearrange("p c k -> p (c k)"),
-                in_=grouped[:].rearrange("p c k t -> p (c k t)"),
-            )
+        def code_tiles(name):
+            codes = work.tile([P, PAIR, PASSES, P], U32, name=name + "_codes", align_bytes=64)
+            scales = work.tile([P, PAIR, PASSES, P], U8, name=name + "_scales", align_bytes=64)
             return codes, scales
 
-        def quantise_q2(n):
-            if 0 <= n < N_TILES:
-                q2_codes[n], q2_scales[n] = quantise_tile(q2_grp[n], "q2")
+        def quantise_tokens(codes, scales, grouped):
+            nc.vector.quantize_mx(
+                out=codes.rearrange("p n c k -> p (n c k)").bitcast(FP8X4),
+                scales=scales.rearrange("p n c k -> p (n c k)"),
+                in_=grouped.rearrange("p n c k t -> p (n c k t)"),
+            )
 
-        def readout(n):
-            if not 0 <= n < N_TILES:
-                return
-            b = n // TILES
-            for half in range(HALVES):
-                t2_bank[n, half] = t2_psum.tile([P, BANK_COLS], F32, name="t2_bank")
-                cols = slice(half * BANK_COLS, (half + 1) * BANK_COLS)
-                for c in range(PASSES):
-                    nc.tensor.matmul_mx(
-                        out=t2_bank[n, half][:],
-                        lhsT=q2_codes[n][:, c, :].bitcast(FP8X4),
-                        lhsT_scale=q2_scales[n][:, c, :],
-                        rhs=kv_codes[b][:, c, cols].bitcast(FP8X4),
-                        rhs_scale=kv_scales[b][:, c, cols],
-                        start=(c == 0),
-                        stop=(c == PASSES - 1),
+        def quantise_q2(p):
+            if 0 <= p < N_PAIRS:
+                q2_codes[p], q2_scales[p] = code_tiles("q2")
+                quantise_tokens(q2_codes[p][:], q2_scales[p][:], q2_grp[p][:])
+
+        def quantise_h(p, first=0, count=PAIR):
+            if 0 <= p < N_PAIRS:
+                if first == 0:
+                    h_codes[p], h_scales[p] = code_tiles("h")
+                tiles = slice(first, first + count)
+                quantise_tokens(h_codes[p][:, tiles], h_scales[p][:, tiles], hT_grp[p][:, tiles])
+
+        def readout(p):
+            for n in pair_tiles(p):
+                b = n // TILES
+                for half in range(HALVES):
+                    t2_bank[n, half] = t2_psum.tile([P, BANK_COLS], F32, name="t2_bank")
+                    cols = slice(half * BANK_COLS, (half + 1) * BANK_COLS)
+                    for c in range(PASSES):
+                        nc.tensor.matmul_mx(
+                            out=t2_bank[n, half][:],
+                            lhsT=q2_codes[p][:, n % PAIR, c, :].bitcast(FP8X4),
+                            lhsT_scale=q2_scales[p][:, n % PAIR, c, :],
+                            rhs=kv_codes[b][:, c, cols].bitcast(FP8X4),
+                            rhs_scale=kv_scales[b][:, c, cols],
+                            start=(c == 0),
+                            stop=(c == PASSES - 1),
+                        )
+
+        def add_values(p, tiles=range(PAIR)):
+            for j in tiles:
+                n = p * PAIR + j
+                g, i = divmod(n, GROUP)
+                if j == 0:
+                    h_nat[p] = work.tile([P, PAIR, FEATS], BF16, name="h_nat")
+                for half in range(HALVES):
+                    cols = slice(half * BANK_COLS, (half + 1) * BANK_COLS)
+                    nc.vector.scalar_tensor_tensor(
+                        out=h_nat[p][:, n % PAIR, cols],
+                        in0=t2_bank[n, half][:],
+                        scalar=1.0 / math.sqrt(TOKENS),
+                        in1=v_nat[g][:, i, cols],
+                        op0=ALU.mult,
+                        op1=ALU.add,
                     )
 
-        def add_values(n):
-            if not 0 <= n < N_TILES:
-                return
-            g, i = divmod(n, GROUP)
-            h_nat[n] = work.tile([P, FEATS], BF16, name="h_nat")
-            for half in range(HALVES):
-                cols = slice(half * BANK_COLS, (half + 1) * BANK_COLS)
-                nc.vector.scalar_tensor_tensor(
-                    out=h_nat[n][:, cols],
-                    in0=t2_bank[n, half][:],
-                    scalar=1.0 / math.sqrt(TOKENS),
-                    in1=v_nat[g][:, i, cols],
-                    op0=ALU.mult,
-                    op1=ALU.add,
-                )
-
-        def quantise_h(n):
-            if 0 <= n < N_TILES:
-                h_codes[n], h_scales[n] = quantise_tile(hT_grp[n], "h")
-
         def project(n):
-            if not 0 <= n < N_TILES:
-                return
-            pair, half = divmod(n, PAIR)
-            if half == 0:
-                out_bank[pair] = out_psum.tile([P, PAIR, OUT_FEATS], F32, name="out_bank")
+            p, half = divmod(n, PAIR)
+            if half == 0 and p < N_PAIRS - 1:
+                out_bank[p] = out_psum.tile([P, PAIR, OUT_FEATS], F32, name="out_bank")
+            elif half == 0:
+                out_bank[p] = t2_psum.tile([P, PAIR, OUT_FEATS], F32, name="t2_bank")
             for c2 in range(PASSES):
                 nc.tensor.matmul_mx(
-                    out=out_bank[pair][:, half, :],
-                    lhsT=h_codes[n][:, c2, :].bitcast(FP8X4),
-                    lhsT_scale=h_scales[n][:, c2, :],
+                    out=out_bank[p][:, half, :],
+                    lhsT=h_codes[p][:, half, c2, :].bitcast(FP8X4),
+                    lhsT_scale=h_scales[p][:, half, c2, :],
                     rhs=w_codes[:, c2, :].bitcast(FP8X4),
                     rhs_scale=w_scales[:, c2, :],
                     start=(c2 == 0),
                     stop=(c2 == PASSES - 1),
                 )
 
-        def add_bias_and_store(n):
-            if not 0 <= n < N_TILES or n % PAIR != PAIR - 1:
+        def add_bias(p, first=0, count=PAIR):
+            if not 0 <= p < N_PAIRS:
                 return
-            out_sb = out_pool.tile([P, PAIR, OUT_FEATS], F32, name="out_sb")
+            if first == 0:
+                out_sb[p] = out_pool.tile([P, PAIR, OUT_FEATS], F32, name="out_sb")
+            tiles = slice(first, first + count)
             nc.vector.tensor_tensor(
-                out=out_sb[:],
-                in0=out_bank[n // PAIR][:],
-                in1=bias[:].unsqueeze(1).to_broadcast([P, PAIR, OUT_FEATS]),
+                out=out_sb[p][:, tiles],
+                in0=out_bank[p][:, tiles],
+                in1=bias[:].unsqueeze(1).to_broadcast([P, count, OUT_FEATS]),
                 op=ALU.add,
             )
-            b, last = divmod(n, TILES)
-            nc.sync.dma_start(out=out_rows[b, :, last + 1 - PAIR : last + 1, :], in_=out_sb[:])
+            b, start = divmod(p * PAIR, TILES)
+            nc.sync.dma_start(
+                out=out_rows[b, :, start + first : start + first + count, :], in_=out_sb[p][:, tiles]
+            )
 
         ctx.enter_context(tc.manual_schedule())
+        vec, sca = nc.vector.tensor_copy, nc.scalar.copy
+
         first_loads()
-        for s in range(FIRST_STEP, LAST_STEP + 1):
-            if s % GROUP == 0:
-                later_loads(s // GROUP + AHEAD_LOADS)
-            project(s - BEHIND_PROJECT)
-            readout(s + AHEAD_READOUT)
-            transpose_q2(s + AHEAD_TRANSPOSE)
-            transpose_h(s - BEHIND_TRANSPOSE)
-            if s + AHEAD_KV_REGROUP < PIECES:
-                regroup_kv(s + AHEAD_KV_REGROUP)
-            sum_squares(s + AHEAD_SUM_SQUARES)
-            copy_q2(s + AHEAD_TRANSPOSE)
-            copy_h(s - BEHIND_TRANSPOSE)
-            regroup_w(s - W_STEP)
-            quantise_kv(s + AHEAD_KV_QUANTISE)
-            if s + AHEAD_KV_REGROUP >= PIECES:
-                regroup_kv(s + AHEAD_KV_REGROUP)
+        regroup_piece(0, vec, first_pool)
+        regroup_piece(1, sca, first_pool)
+        regroup_piece(2, sca, first_pool)
+        regroup_piece(3, vec, first_pool)
+        sum_squares(0)
+        quantise_kv(0)
+        regroup_piece(4, vec, first_pool)
+        quantise_kv(1)
+        regroup_piece(5, vec, first_pool)
+        floor_norms(0)
+        invert_norms(0)
+        normalise(0)
+        normalise(1)
+        transpose_q2(0)
+        regroup_piece(6, vec, part_pool)
+        sum_squares(1)
+        copy_q2(0)
+        regroup_piece(7, vec, part_pool)
+        quantise_kv(2)
+        floor_norms(1)
+        quantise_q2(0)
+        invert_norms(1)
+        quantise_kv(3)
+        normalise(2)
+        regroup_part(KV_PARTS + 1)
+        normalise(3)
+        readout(0)
+        transpose_q2(1)
+        sum_squares(2)
+        copy_q2(1)
+        later_loads(2)
+
+        for s in range(N_PAIRS - 1):
+            if s > 0 and s % 2 == 0:
+                later_loads(s // 2 + 2)
+            for n in pair_tiles(s - 1):
+                transpose_h(n)
+            if s > 0:
+                transpose_q2(s + 2)
+            sum_squares(s + 3)
+            for n in pair_tiles(s - 1):
+                copy_h(n)
+            if s > 0:
+                copy_q2(s + 2)
             add_values(s)
-            add_bias_and_store(s - BEHIND_PROJECT)
-            normalise(s + AHEAD_NORMALISE)
-            quantise_w(s - W_STEP - 1)
-            quantise_q2(s + AHEAD_QUANTISE_Q2)
-            quantise_h(s - BEHIND_QUANTISE_H)
-            invert_norms(s + AHEAD_SUM_SQUARES)
+            add_bias(s - 2)
+            if s == 0:
+                regroup_piece(8, vec, first_pool)
+                floor_norms(2)
+                quantise_q2(1)
+                invert_norms(2)
+                readout(1)
+                regroup_piece(9, vec, first_pool)
+                normalise(4)
+                normalise(5)
+                transpose_q2(2)
+                copy_q2(2)
+                quantise_kv(KV_PARTS)
+                regroup_w(0)
+                floor_norms(3)
+                regroup_w(1)
+                invert_norms(3)
+            else:
+                quantise_q2(s + 1)
+                readout(s + 1)
+                floor_norms(s + 3)
+                quantise_h(s - 1)
+                if s == 1:
+                    quantise_w()
+                invert_norms(s + 3)
+            if s < N_PAIRS - 2:
+                for n in pair_tiles(s - 1):
+                    project(n)
+            normalise((s + 3) * PAIR)
+            quantise_kv(s + KV_PARTS + 1)
+            normalise((s + 3) * PAIR + 1)
+            regroup_part(s + KV_PARTS + 2)
+        last = N_PAIRS - 1
+        for n in pair_tiles(last - 1):
+            transpose_h(n)
+            copy_h(n)
+        for n in pair_tiles(last - 2):
+            project(n)
+        add_values(last, (0,))
+        transpose_h(N_TILES - 2)
+        copy_h(N_TILES - 2)
+        add_values(last, (1,))
+        transpose_h(N_TILES - 1)
+        copy_h(N_TILES - 1)
+        quantise_h(last - 1)
+        add_bias(last - 2)
+        for n in pair_tiles(last - 1):
+            project(n)
+        quantise_h(last, 0, 1)
+        add_bias(last - 1)
+        project(N_TILES - 2)
+        quantise_h(last, 1, 1)
+        add_bias(last, 0, 1)
+        project(N_TILES - 1)
+        add_bias(last, 1, 1)

@@ -13,7 +13,7 @@ ALU = mybir.AluOpType
 ACT = mybir.ActivationFunctionType
 
 BATCH, TOKENS, FEATS, OUT_FEATS = 4, 1024, 1024, 256
-EPS_NORM = 1e-12
+EPS_SQUARED = 1e-12**2
 FLOPS = 2 * BATCH * TOKENS * FEATS * FEATS + 2 * BATCH * TOKENS * FEATS * OUT_FEATS
 
 P = 128
@@ -51,7 +51,8 @@ def tile_essattn_pb_t_kernel(tc, q_feat, kv, v, w_proj, b_proj, out):
         const = ctx.enter_context(tc.tile_pool(name="const", bufs=1))
         q_pool = ctx.enter_context(tc.tile_pool(name="q_nat", bufs=4))
         v_pool = ctx.enter_context(tc.tile_pool(name="v_nat", bufs=4))
-        kv_raw_pool = ctx.enter_context(tc.tile_pool(name="kv_raw", bufs=4))
+        kv_head_pool = ctx.enter_context(tc.tile_pool(name="kv_head", bufs=KV_PARTS))
+        kv_raw_pool = ctx.enter_context(tc.tile_pool(name="kv_raw", bufs=3))
         part_pool = ctx.enter_context(tc.tile_pool(name="kv_part", bufs=1))
         first_pool = ctx.enter_context(tc.tile_pool(name="kv_first", bufs=3))
         kv_pool = ctx.enter_context(tc.tile_pool(name="kv", bufs=2))
@@ -61,8 +62,8 @@ def tile_essattn_pb_t_kernel(tc, q_feat, kv, v, w_proj, b_proj, out):
         t2_psum = ctx.enter_context(tc.psum_pool(name="t2_psum", bufs=4))
         out_psum = ctx.enter_context(tc.psum_pool(name="out_psum", bufs=1))
 
-        q_nat, v_nat, kv_raw, kv_grp, kv_codes, kv_scales = {}, {}, {}, {}, {}, {}
-        sumsq, norm, floored, inv_norm = {}, {}, {}, {}
+        q_nat, v_nat, kv_head, kv_raw, kv_grp, kv_codes, kv_scales = {}, {}, {}, {}, {}, {}, {}
+        sumsq, excess, inv_norm = {}, {}, {}
         q2_nat, q2_bank, q2_grp, q2_codes, q2_scales = {}, {}, {}, {}, {}
         t2_bank, h_nat, h_bank, hT_grp, h_codes, h_scales = {}, {}, {}, {}, {}, {}
         out_bank, out_sb = {}, {}
@@ -73,7 +74,7 @@ def tile_essattn_pb_t_kernel(tc, q_feat, kv, v, w_proj, b_proj, out):
         one = const.tile([P, 1], F32, name="one")
         one_root = const.tile([P, 1], F32, name="one_root")
         nc.vector.memset(one[:], 1.0)
-        nc.scalar.sqrt(one_root[:], one[:])
+        nc.scalar.activation(out=one_root[:], in_=one[:], func=ACT.Abs_reciprocal_sqrt)
 
         w_raw = const.tile([P, PASSES, PACK, OUT_FEATS], BF16, name="w_raw")
         w_grp = const.tile([P, PASSES, OUT_FEATS, PACK], BF16, name="w_grp", align_bytes=64)
@@ -81,23 +82,21 @@ def tile_essattn_pb_t_kernel(tc, q_feat, kv, v, w_proj, b_proj, out):
         w_scales = const.tile([P, PASSES, OUT_FEATS], U8, name="w_scales", align_bytes=64)
         bias = const.tile([P, OUT_FEATS], BF16, name="bias")
 
-        def load_kv(half, parts=1, which=(0, 1)):
-            b, c = divmod(half, PASSES)
-            if half not in kv_raw:
-                kv_raw[half] = kv_raw_pool.tile([P, PACK, FEATS], BF16, name="kv_raw")
-            if parts == 1:
+        def load_kv_part(part):
+            c, a = divmod(part, FEATS // HALF_COLS)
+            cols = slice(a * HALF_COLS, (a + 1) * HALF_COLS)
+            kv_head[part] = kv_head_pool.tile([P, PACK, HALF_COLS], BF16, name="kv_head")
+            for u in range(2):
                 nc.sync.dma_start(
-                    out=kv_raw[half][:].rearrange("p (u e) w -> p u (e w)", e=2), in_=kv_rows[b, c]
+                    out=kv_head[part][:, 2 * u : 2 * u + 2, :], in_=kv_part_rows[0, c, :, u, :, cols]
                 )
-                return
-            width = FEATS // parts
-            for part in which:
-                cols = slice(part * width, (part + 1) * width)
-                for u in range(2):
-                    nc.sync.dma_start(
-                        out=kv_raw[half][:, 2 * u : 2 * u + 2, cols],
-                        in_=kv_part_rows[b, c, :, u, :, cols],
-                    )
+
+        def load_kv(half):
+            b, c = divmod(half, PASSES)
+            kv_raw[half] = kv_raw_pool.tile([P, PACK, FEATS], BF16, name="kv_raw")
+            nc.sync.dma_start(
+                out=kv_raw[half][:].rearrange("p (u e) w -> p u (e w)", e=2), in_=kv_rows[b, c]
+            )
 
         def load_tokens(tiles, pool, rows, g, name, first=0, count=GROUP):
             b, start = divmod(g * GROUP, TILES)
@@ -109,11 +108,12 @@ def tile_essattn_pb_t_kernel(tc, q_feat, kv, v, w_proj, b_proj, out):
             )
 
         def first_loads():
-            load_kv(0, parts=2)
+            load_kv_part(0)
+            load_kv_part(1)
             load_tokens(q_nat, q_pool, q_rows, 0, "q_nat", 0, PAIR)
-            load_kv(1, parts=2, which=(0,))
+            load_kv_part(2)
             load_tokens(q_nat, q_pool, q_rows, 0, "q_nat", PAIR, PAIR)
-            load_kv(1, parts=2, which=(1,))
+            load_kv_part(3)
             load_tokens(v_nat, v_pool, v_rows, 0, "v_nat", 0, PAIR)
             load_tokens(q_nat, q_pool, q_rows, 1, "q_nat", 0, PAIR)
             load_kv(2)
@@ -135,16 +135,18 @@ def tile_essattn_pb_t_kernel(tc, q_feat, kv, v, w_proj, b_proj, out):
 
         def regroup_piece(k, copy, pool):
             part, i = divmod(k, HALF_COLS // PIECE_COLS)
-            c, a = divmod(k, FEATS // PIECE_COLS)
+            if part < KV_PARTS:
+                source = kv_head[part][:, :, i * PIECE_COLS : (i + 1) * PIECE_COLS]
+            else:
+                half, a = divmod(k, FEATS // PIECE_COLS)
+                source = kv_raw[half][:, :, a * PIECE_COLS : (a + 1) * PIECE_COLS]
             if i == 0:
                 kv_grp[part] = pool.tile([P, HALF_COLS, PACK], BF16, name="kv_part", align_bytes=64)
             copy(
                 out=kv_grp[part][:, i * PIECE_COLS : (i + 1) * PIECE_COLS, :].rearrange(
                     "p (c i) t -> p c t i", i=RUN
                 ),
-                in_=kv_raw[c][:, :, a * PIECE_COLS : (a + 1) * PIECE_COLS].rearrange(
-                    "p t (c i) -> p c t i", i=RUN
-                ),
+                in_=source.rearrange("p t (c i) -> p c t i", i=RUN),
             )
 
         def regroup_part(k):
@@ -201,19 +203,18 @@ def tile_essattn_pb_t_kernel(tc, q_feat, kv, v, w_proj, b_proj, out):
                     func=ACT.Square,
                     accum_out=sumsq[p][:, n % PAIR : n % PAIR + 1],
                 )
-                if n % PAIR == PAIR - 1:
-                    norm[p] = work.tile([P, PAIR], F32, name="norm")
-                    nc.scalar.sqrt(norm[p][:], sumsq[p][:])
 
-        def floor_norms(p):
+        def floor_squares(p):
             if 0 <= p < N_PAIRS:
-                floored[p] = work.tile([P, PAIR], F32, name="floored")
-                nc.vector.tensor_scalar_max(out=floored[p][:], in0=norm[p][:], scalar1=EPS_NORM)
+                excess[p] = work.tile([P, PAIR], F32, name="excess")
+                nc.scalar.activation(out=excess[p][:], in_=sumsq[p][:], func=ACT.Relu, bias=-EPS_SQUARED)
 
         def invert_norms(p):
             if 0 <= p < N_PAIRS:
                 inv_norm[p] = work.tile([P, PAIR], F32, name="inv_norm")
-                nc.vector.reciprocal(out=inv_norm[p][:], in_=floored[p][:])
+                nc.scalar.activation(
+                    out=inv_norm[p][:], in_=excess[p][:], func=ACT.Abs_reciprocal_sqrt, bias=EPS_SQUARED
+                )
 
         def normalise(n):
             if not 0 <= n < N_TILES:
@@ -246,11 +247,13 @@ def tile_essattn_pb_t_kernel(tc, q_feat, kv, v, w_proj, b_proj, out):
             for n in pair_tiles(p):
                 q2_bank[n] = turn(q2_nat[p][:, n % PAIR, :])
 
-        def copy_q2(p):
-            if 0 <= p < N_PAIRS:
+        def copy_q2(n):
+            if not 0 <= n < N_TILES:
+                return
+            p, half = divmod(n, PAIR)
+            if half == 0:
                 q2_grp[p] = work.tile([P, PAIR, PASSES, P, PACK], BF16, name="q2_grp", align_bytes=64)
-            for n in pair_tiles(p):
-                copy_turned(q2_bank[n], q2_grp[p][:, n % PAIR])
+            copy_turned(q2_bank[n], q2_grp[p][:, half])
 
         def transpose_h(n):
             h_bank[n] = turn(h_nat[n // PAIR][:, n % PAIR, :])
@@ -362,32 +365,38 @@ def tile_essattn_pb_t_kernel(tc, q_feat, kv, v, w_proj, b_proj, out):
         regroup_piece(2, sca, first_pool)
         regroup_piece(3, vec, first_pool)
         sum_squares(0)
+        floor_squares(0)
+        invert_norms(0)
         quantise_kv(0)
         regroup_piece(4, vec, first_pool)
         quantise_kv(1)
         regroup_piece(5, vec, first_pool)
-        floor_norms(0)
-        invert_norms(0)
         normalise(0)
         normalise(1)
         transpose_q2(0)
         regroup_piece(6, vec, part_pool)
         sum_squares(1)
+        floor_squares(1)
         copy_q2(0)
+        invert_norms(1)
+        copy_q2(1)
         regroup_piece(7, vec, part_pool)
         quantise_kv(2)
-        floor_norms(1)
-        quantise_q2(0)
-        invert_norms(1)
-        quantise_kv(3)
         normalise(2)
-        regroup_part(KV_PARTS + 1)
         normalise(3)
-        readout(0)
         transpose_q2(1)
+        quantise_q2(0)
+        quantise_kv(3)
+        regroup_part(KV_PARTS + 1)
+        readout(0)
         sum_squares(2)
-        copy_q2(1)
+        floor_squares(2)
+        copy_q2(2)
+        invert_norms(2)
+        copy_q2(3)
         later_loads(2)
+        sum_squares(3)
+        floor_squares(3)
 
         for s in range(N_PAIRS - 1):
             if s > 0 and s % 2 == 0:
@@ -396,37 +405,38 @@ def tile_essattn_pb_t_kernel(tc, q_feat, kv, v, w_proj, b_proj, out):
                 transpose_h(n)
             if s > 0:
                 transpose_q2(s + 2)
-            sum_squares(s + 3)
-            for n in pair_tiles(s - 1):
-                copy_h(n)
-            if s > 0:
-                copy_q2(s + 2)
+                for n in pair_tiles(s - 1):
+                    copy_h(n)
+                sum_squares(s + 4)
+                copy_q2((s + 2) * PAIR)
+                floor_squares(s + 4)
+                copy_q2((s + 2) * PAIR + 1)
+                invert_norms(s + 4)
             add_values(s)
             add_bias(s - 2)
             if s == 0:
                 regroup_piece(8, vec, first_pool)
-                floor_norms(2)
-                quantise_q2(1)
-                invert_norms(2)
-                readout(1)
-                regroup_piece(9, vec, first_pool)
                 normalise(4)
                 normalise(5)
                 transpose_q2(2)
-                copy_q2(2)
+                quantise_q2(1)
+                readout(1)
+                regroup_piece(9, vec, first_pool)
+                copy_q2(4)
+                invert_norms(3)
+                copy_q2(5)
+                sum_squares(4)
+                floor_squares(4)
+                invert_norms(4)
                 quantise_kv(KV_PARTS)
                 regroup_w(0)
-                floor_norms(3)
                 regroup_w(1)
-                invert_norms(3)
             else:
                 quantise_q2(s + 1)
                 readout(s + 1)
-                floor_norms(s + 3)
                 quantise_h(s - 1)
                 if s == 1:
                     quantise_w()
-                invert_norms(s + 3)
             if s < N_PAIRS - 2:
                 for n in pair_tiles(s - 1):
                     project(n)

@@ -288,9 +288,9 @@ def tile_essattn_pb_t_kernel(tc, q_feat, kv, v, w_proj, b_proj, out):
                 tiles = slice(first, first + count)
                 quantise_tokens(h_codes[p][:, tiles], h_scales[p][:, tiles], hT_grp[p][:, tiles])
 
-        def readout(p):
-            for n in pair_tiles(p):
-                b = n // TILES
+        def readout(n):
+            if 0 <= n < N_TILES:
+                p, b = n // PAIR, n // TILES
                 for half in range(HALVES):
                     t2_bank[n, half] = t2_psum.tile([P, BANK_COLS], F32, name="t2_bank")
                     cols = slice(half * BANK_COLS, (half + 1) * BANK_COLS)
@@ -305,26 +305,25 @@ def tile_essattn_pb_t_kernel(tc, q_feat, kv, v, w_proj, b_proj, out):
                             stop=(c == PASSES - 1),
                         )
 
-        def add_values(p, tiles=range(PAIR)):
-            for j in tiles:
-                n = p * PAIR + j
-                g, i = divmod(n, GROUP)
-                if j == 0:
-                    h_nat[p] = work.tile([P, PAIR, FEATS], BF16, name="h_nat")
-                for half in range(HALVES):
-                    cols = slice(half * BANK_COLS, (half + 1) * BANK_COLS)
-                    nc.vector.scalar_tensor_tensor(
-                        out=h_nat[p][:, n % PAIR, cols],
-                        in0=t2_bank[n, half][:],
-                        scalar=1.0 / math.sqrt(TOKENS),
-                        in1=v_nat[g][:, i, cols],
-                        op0=ALU.mult,
-                        op1=ALU.add,
-                    )
+        def add_values(n):
+            g, i = divmod(n, GROUP)
+            p, j = divmod(n, PAIR)
+            if j == 0:
+                h_nat[p] = work.tile([P, PAIR, FEATS], BF16, name="h_nat")
+            for half in range(HALVES):
+                cols = slice(half * BANK_COLS, (half + 1) * BANK_COLS)
+                nc.vector.scalar_tensor_tensor(
+                    out=h_nat[p][:, j, cols],
+                    in0=t2_bank[n, half][:],
+                    scalar=1.0 / math.sqrt(TOKENS),
+                    in1=v_nat[g][:, i, cols],
+                    op0=ALU.mult,
+                    op1=ALU.add,
+                )
 
         def project(n):
             p, half = divmod(n, PAIR)
-            if half == 0 and p < N_PAIRS - 1:
+            if half == 0 and p < N_PAIRS - 2:
                 out_bank[p] = out_psum.tile([P, PAIR, OUT_FEATS], F32, name="out_bank")
             elif half == 0:
                 out_bank[p] = t2_psum.tile([P, PAIR, OUT_FEATS], F32, name="t2_bank")
@@ -389,6 +388,7 @@ def tile_essattn_pb_t_kernel(tc, q_feat, kv, v, w_proj, b_proj, out):
         quantise_kv(3)
         regroup_part(KV_PARTS + 1)
         readout(0)
+        readout(1)
         sum_squares(2)
         floor_squares(2)
         copy_q2(2)
@@ -401,69 +401,66 @@ def tile_essattn_pb_t_kernel(tc, q_feat, kv, v, w_proj, b_proj, out):
         for s in range(N_PAIRS - 1):
             if s > 0 and s % 2 == 0:
                 later_loads(s // 2 + 2)
-            for n in pair_tiles(s - 1):
-                transpose_h(n)
+            add_bias(s - 3)
             if s > 0:
                 transpose_q2(s + 2)
-                for n in pair_tiles(s - 1):
-                    copy_h(n)
-                sum_squares(s + 4)
-                copy_q2((s + 2) * PAIR)
-                floor_squares(s + 4)
-                copy_q2((s + 2) * PAIR + 1)
-                invert_norms(s + 4)
-            add_values(s)
-            add_bias(s - 2)
+                for n in pair_tiles(s + 2):
+                    copy_q2(n)
+            for n in pair_tiles(s - 2):
+                project(n)
+            for n in pair_tiles(s):
+                add_values(n)
             if s == 0:
                 regroup_piece(8, vec, first_pool)
                 normalise(4)
                 normalise(5)
                 transpose_q2(2)
                 quantise_q2(1)
-                readout(1)
+                for n in pair_tiles(2):
+                    copy_q2(n)
                 regroup_piece(9, vec, first_pool)
-                copy_q2(4)
                 invert_norms(3)
-                copy_q2(5)
-                sum_squares(4)
-                floor_squares(4)
-                invert_norms(4)
                 quantise_kv(KV_PARTS)
                 regroup_w(0)
                 regroup_w(1)
             else:
                 quantise_q2(s + 1)
-                readout(s + 1)
-                quantise_h(s - 1)
-                if s == 1:
-                    quantise_w()
-            if s < N_PAIRS - 2:
-                for n in pair_tiles(s - 1):
-                    project(n)
+            sum_squares(s + 4)
+            for n in pair_tiles(s):
+                transpose_h(n)
+            first, second = pair_tiles(s)
+            copy_h(first)
+            floor_squares(s + 4)
+            copy_h(second)
+            invert_norms(s + 4)
+            for n in pair_tiles(s + 1):
+                readout(n)
             normalise((s + 3) * PAIR)
-            quantise_kv(s + KV_PARTS + 1)
             normalise((s + 3) * PAIR + 1)
+            if s == 1:
+                quantise_w()
+            quantise_kv(s + KV_PARTS + 1)
             regroup_part(s + KV_PARTS + 2)
+            quantise_h(s - 1)
         last = N_PAIRS - 1
-        for n in pair_tiles(last - 1):
-            transpose_h(n)
-            copy_h(n)
+        first, second = pair_tiles(last)
+        add_bias(last - 3)
         for n in pair_tiles(last - 2):
             project(n)
-        add_values(last, (0,))
-        transpose_h(N_TILES - 2)
-        copy_h(N_TILES - 2)
-        add_values(last, (1,))
-        transpose_h(N_TILES - 1)
-        copy_h(N_TILES - 1)
+        add_values(first)
+        transpose_h(first)
+        copy_h(first)
+        add_values(second)
+        transpose_h(second)
+        copy_h(second)
         quantise_h(last - 1)
         add_bias(last - 2)
         for n in pair_tiles(last - 1):
             project(n)
         quantise_h(last, 0, 1)
-        add_bias(last - 1)
-        project(N_TILES - 2)
         quantise_h(last, 1, 1)
+        add_bias(last - 1)
+        project(first)
         add_bias(last, 0, 1)
-        project(N_TILES - 1)
+        project(second)
         add_bias(last, 1, 1)

@@ -116,12 +116,12 @@ def tile_essattn_pb_t_kernel(tc, q_feat, kv, v, w_proj, b_proj, out):
             load_kv_part(3)
             load_tokens(v_nat, v_pool, v_rows, 0, "v_nat", 0, PAIR)
             load_tokens(q_nat, q_pool, q_rows, 1, "q_nat", 0, PAIR)
-            load_kv(2)
-            load_tokens(v_nat, v_pool, v_rows, 0, "v_nat", PAIR, PAIR)
-            load_tokens(q_nat, q_pool, q_rows, 1, "q_nat", PAIR, PAIR)
             nc.sync.dma_start(
                 out=w_raw[:].rearrange("p c (u e) n -> p (c u) (e n)", e=2), in_=w_rows
             )
+            load_kv(2)
+            load_tokens(q_nat, q_pool, q_rows, 1, "q_nat", PAIR, PAIR)
+            load_tokens(v_nat, v_pool, v_rows, 0, "v_nat", PAIR, PAIR)
             nc.sync.dma_start(out=bias[:], in_=b_proj.partition_broadcast(P))
             load_kv(3)
 
@@ -191,18 +191,20 @@ def tile_essattn_pb_t_kernel(tc, q_feat, kv, v, w_proj, b_proj, out):
         def pair_tiles(p):
             return range(p * PAIR, (p + 1) * PAIR) if 0 <= p < N_PAIRS else ()
 
-        def sum_squares(p):
-            for n in pair_tiles(p):
-                g, i = divmod(n, GROUP)
-                if n % PAIR == 0:
-                    sumsq[p] = work.tile([P, PAIR], F32, name="sumsq")
-                squares = work.tile([P, FEATS], BF16, name="squares")
-                nc.scalar.activation(
-                    out=squares[:],
-                    in_=q_nat[g][:, i, :],
-                    func=ACT.Square,
-                    accum_out=sumsq[p][:, n % PAIR : n % PAIR + 1],
-                )
+        def sum_squares(n):
+            if not 0 <= n < N_TILES:
+                return
+            g, i = divmod(n, GROUP)
+            p, j = divmod(n, PAIR)
+            if j == 0:
+                sumsq[p] = work.tile([P, PAIR], F32, name="sumsq")
+            squares = work.tile([P, FEATS], BF16, name="squares")
+            nc.scalar.activation(
+                out=squares[:],
+                in_=q_nat[g][:, i, :],
+                func=ACT.Square,
+                accum_out=sumsq[p][:, j : j + 1],
+            )
 
         def floor_squares(p):
             if 0 <= p < N_PAIRS:
@@ -364,6 +366,7 @@ def tile_essattn_pb_t_kernel(tc, q_feat, kv, v, w_proj, b_proj, out):
         regroup_piece(2, sca, first_pool)
         regroup_piece(3, vec, first_pool)
         sum_squares(0)
+        sum_squares(1)
         floor_squares(0)
         invert_norms(0)
         quantise_kv(0)
@@ -374,7 +377,8 @@ def tile_essattn_pb_t_kernel(tc, q_feat, kv, v, w_proj, b_proj, out):
         normalise(1)
         transpose_q2(0)
         regroup_piece(6, vec, part_pool)
-        sum_squares(1)
+        sum_squares(2)
+        sum_squares(3)
         floor_squares(1)
         copy_q2(0)
         invert_norms(1)
@@ -385,18 +389,19 @@ def tile_essattn_pb_t_kernel(tc, q_feat, kv, v, w_proj, b_proj, out):
         normalise(3)
         transpose_q2(1)
         quantise_q2(0)
+        regroup_w(0)
         quantise_kv(3)
         regroup_part(KV_PARTS + 1)
+        regroup_w(1)
         readout(0)
         readout(1)
-        sum_squares(2)
+        sum_squares(4)
+        sum_squares(5)
         floor_squares(2)
         copy_q2(2)
         invert_norms(2)
         copy_q2(3)
         later_loads(2)
-        sum_squares(3)
-        floor_squares(3)
 
         for s in range(N_PAIRS - 1):
             if s > 0 and s % 2 == 0:
@@ -404,35 +409,31 @@ def tile_essattn_pb_t_kernel(tc, q_feat, kv, v, w_proj, b_proj, out):
             add_bias(s - 3)
             if s > 0:
                 transpose_q2(s + 2)
-                for n in pair_tiles(s + 2):
-                    copy_q2(n)
             for n in pair_tiles(s - 2):
                 project(n)
             for n in pair_tiles(s):
                 add_values(n)
             if s == 0:
-                regroup_piece(8, vec, first_pool)
+                regroup_piece(8, sca, first_pool)
+            for n in pair_tiles(s + 3):
+                sum_squares(n)
+            if s == 0:
                 normalise(4)
                 normalise(5)
                 transpose_q2(2)
+            floor_squares(s + 3)
+            copy_q2((s + 2) * PAIR)
+            invert_norms(s + 3)
+            copy_q2((s + 2) * PAIR + 1)
+            if s == 0:
                 quantise_q2(1)
-                for n in pair_tiles(2):
-                    copy_q2(n)
                 regroup_piece(9, vec, first_pool)
-                invert_norms(3)
                 quantise_kv(KV_PARTS)
-                regroup_w(0)
-                regroup_w(1)
             else:
                 quantise_q2(s + 1)
-            sum_squares(s + 4)
             for n in pair_tiles(s):
                 transpose_h(n)
-            first, second = pair_tiles(s)
-            copy_h(first)
-            floor_squares(s + 4)
-            copy_h(second)
-            invert_norms(s + 4)
+                copy_h(n)
             for n in pair_tiles(s + 1):
                 readout(n)
             normalise((s + 3) * PAIR)

@@ -33,6 +33,7 @@ BATCH_PAIRS = TILES // PAIR
 
 HALF_COLS = FEATS // 2
 KV_PARTS = PASSES * FEATS // HALF_COLS
+GPSIMD_COLS = 448
 PIECE_COLS = HALF_COLS // 2
 RUN = 4
 
@@ -116,14 +117,18 @@ def tile_essattn_pb_t_kernel(tc, q_feat, kv, v, w_proj, b_proj, out):
             load_kv_part(3)
             load_tokens(v_nat, v_pool, v_rows, 0, "v_nat", 0, PAIR)
             load_tokens(q_nat, q_pool, q_rows, 1, "q_nat", 0, PAIR)
-            nc.sync.dma_start(
-                out=w_raw[:].rearrange("p c (u e) n -> p (c u) (e n)", e=2), in_=w_rows
-            )
             load_kv(2)
             load_tokens(q_nat, q_pool, q_rows, 1, "q_nat", PAIR, PAIR)
             load_tokens(v_nat, v_pool, v_rows, 0, "v_nat", PAIR, PAIR)
             nc.sync.dma_start(out=bias[:], in_=b_proj.partition_broadcast(P))
             load_kv(3)
+            load_tokens(q_nat, q_pool, q_rows, 2, "q_nat", 0, PAIR)
+            nc.sync.dma_start(
+                out=w_raw[:].rearrange("p c (u e) n -> p (c u) (e n)", e=2), in_=w_rows
+            )
+            load_tokens(q_nat, q_pool, q_rows, 2, "q_nat", PAIR, PAIR)
+            load_tokens(v_nat, v_pool, v_rows, 1, "v_nat")
+            load_kv(4)
 
         def later_loads(g):
             if g < N_GROUPS:
@@ -154,13 +159,24 @@ def tile_essattn_pb_t_kernel(tc, q_feat, kv, v, w_proj, b_proj, out):
                 return
             half, a = divmod(k, FEATS // HALF_COLS)
             kv_grp[k] = part_pool.tile([P, HALF_COLS, PACK], BF16, name="kv_part", align_bytes=64)
+            cols = slice(a * HALF_COLS, a * HALF_COLS + GPSIMD_COLS)
             nc.gpsimd.tensor_scalar(
-                out=kv_grp[k][:],
-                in0=kv_raw[half][:, :, a * HALF_COLS : (a + 1) * HALF_COLS].rearrange("p t m -> p m t"),
+                out=kv_grp[k][:, :GPSIMD_COLS],
+                in0=kv_raw[half][:, :, cols].rearrange("p t m -> p m t"),
                 scalar1=1.0,
                 scalar2=0.0,
                 op0=ALU.mult,
                 op1=ALU.add,
+            )
+
+        def regroup_rest(k):
+            if k >= BATCH * KV_PARTS:
+                return
+            half, a = divmod(k, FEATS // HALF_COLS)
+            cols = slice(a * HALF_COLS + GPSIMD_COLS, (a + 1) * HALF_COLS)
+            nc.scalar.copy(
+                out=kv_grp[k][:, GPSIMD_COLS:].rearrange("p (c i) t -> p c t i", i=RUN),
+                in_=kv_raw[half][:, :, cols].rearrange("p t (c i) -> p c t i", i=RUN),
             )
 
         def quantise_kv(k):
@@ -389,10 +405,8 @@ def tile_essattn_pb_t_kernel(tc, q_feat, kv, v, w_proj, b_proj, out):
         normalise(3)
         transpose_q2(1)
         quantise_q2(0)
-        regroup_w(0)
         quantise_kv(3)
         regroup_part(KV_PARTS + 1)
-        regroup_w(1)
         readout(0)
         readout(1)
         sum_squares(4)
@@ -401,7 +415,6 @@ def tile_essattn_pb_t_kernel(tc, q_feat, kv, v, w_proj, b_proj, out):
         copy_q2(2)
         invert_norms(2)
         copy_q2(3)
-        later_loads(2)
 
         for s in range(N_PAIRS - 1):
             if s > 0 and s % 2 == 0:
@@ -425,6 +438,7 @@ def tile_essattn_pb_t_kernel(tc, q_feat, kv, v, w_proj, b_proj, out):
             copy_q2((s + 2) * PAIR)
             invert_norms(s + 3)
             copy_q2((s + 2) * PAIR + 1)
+            regroup_rest(s + KV_PARTS + 1)
             if s == 0:
                 quantise_q2(1)
                 regroup_piece(9, vec, first_pool)
@@ -436,6 +450,9 @@ def tile_essattn_pb_t_kernel(tc, q_feat, kv, v, w_proj, b_proj, out):
                 copy_h(n)
             for n in pair_tiles(s + 1):
                 readout(n)
+            if s == 1:
+                regroup_w(0)
+                regroup_w(1)
             normalise((s + 3) * PAIR)
             normalise((s + 3) * PAIR + 1)
             if s == 1:

import math
from contextlib import ExitStack

import concourse.mybir as mybir
from concourse.masks import make_identity

BF16 = mybir.dt.bfloat16
F32 = mybir.dt.float32
U32 = mybir.dt.uint32
U8 = mybir.dt.uint8
FP8X4 = mybir.dt.float8_e4m3fn_x4
ALU = mybir.AluOpType
ACT = mybir.ActivationFunctionType

BATCH, TOKENS, FEATS, OUT_FEATS = 4, 1024, 1024, 256
EPS_SQUARED = 1e-12**2
FLOPS = 2 * BATCH * TOKENS * FEATS * FEATS + 2 * BATCH * TOKENS * FEATS * OUT_FEATS

P = 128
PACK = 4
PASSES = FEATS // (P * PACK)
WORD_BLOCKS = FEATS // (2 * P)
BANK_COLS = 512
HALVES = FEATS // BANK_COLS

TILES = TOKENS // P
N_TILES = BATCH * TILES
GROUP = 4
N_GROUPS = N_TILES // GROUP
PAIR = 2
N_PAIRS = N_TILES // PAIR
BATCH_PAIRS = TILES // PAIR

HALF_COLS = FEATS // 2
KV_PARTS = PASSES * FEATS // HALF_COLS
GPSIMD_COLS = 448
PIECE_COLS = HALF_COLS // 2
RUN = 4


def tile_essattn_pb_t_kernel(tc, q_feat, kv, v, w_proj, b_proj, out):
    nc = tc.nc

    q_rows = q_feat.rearrange("b (p t) f -> b p t f", t=TILES)
    v_rows = v.rearrange("b (p t) f -> b p t f", t=TILES)
    out_rows = out.rearrange("b (p t) n -> b p t n", t=TILES)
    kv_rows = kv.rearrange("b (c u p e) w -> b c p u (e w)", c=PASSES, p=P, e=2)
    kv_part_rows = kv.rearrange("b (c u p e) w -> b c p u e w", c=PASSES, p=P, e=2)
    w_rows = w_proj.rearrange("(cu p e) n -> p cu (e n)", p=P, e=2)

    with ExitStack() as ctx:
        const = ctx.enter_context(tc.tile_pool(name="const", bufs=1))
        q_pool = ctx.enter_context(tc.tile_pool(name="q_nat", bufs=4))
        v_pool = ctx.enter_context(tc.tile_pool(name="v_nat", bufs=4))
        kv_head_pool = ctx.enter_context(tc.tile_pool(name="kv_head", bufs=KV_PARTS))
        kv_raw_pool = ctx.enter_context(tc.tile_pool(name="kv_raw", bufs=3))
        part_pool = ctx.enter_context(tc.tile_pool(name="kv_part", bufs=1))
        first_pool = ctx.enter_context(tc.tile_pool(name="kv_first", bufs=3))
        kv_pool = ctx.enter_context(tc.tile_pool(name="kv", bufs=2))
        work = ctx.enter_context(tc.tile_pool(name="work", bufs=3))
        out_pool = ctx.enter_context(tc.tile_pool(name="out", bufs=3))
        turn_psum = ctx.enter_context(tc.psum_pool(name="turn_psum", bufs=3))
        t2_psum = ctx.enter_context(tc.psum_pool(name="t2_psum", bufs=4))
        out_psum = ctx.enter_context(tc.psum_pool(name="out_psum", bufs=1))

        q_nat, v_nat, kv_head, kv_raw, kv_grp, kv_codes, kv_scales = {}, {}, {}, {}, {}, {}, {}
        sumsq, excess, inv_norm = {}, {}, {}
        q2_nat, q2_bank, q2_grp, q2_codes, q2_scales = {}, {}, {}, {}, {}
        t2_bank, h_nat, h_bank, hT_grp, h_codes, h_scales = {}, {}, {}, {}, {}, {}
        out_bank, out_sb = {}, {}

        ident = const.tile([P, P], F32, name="ident")
        make_identity(nc, ident[:])

        one = const.tile([P, 1], F32, name="one")
        one_root = const.tile([P, 1], F32, name="one_root")
        nc.vector.memset(one[:], 1.0)
        nc.scalar.activation(out=one_root[:], in_=one[:], func=ACT.Abs_reciprocal_sqrt)

        w_raw = const.tile([P, PASSES, PACK, OUT_FEATS], BF16, name="w_raw")
        w_grp = const.tile([P, PASSES, OUT_FEATS, PACK], BF16, name="w_grp", align_bytes=64)
        w_codes = const.tile([P, PASSES, OUT_FEATS], U32, name="w_codes", align_bytes=64)
        w_scales = const.tile([P, PASSES, OUT_FEATS], U8, name="w_scales", align_bytes=64)
        bias = const.tile([P, OUT_FEATS], BF16, name="bias")

        def load_kv_part(part):
            c, a = divmod(part, FEATS // HALF_COLS)
            cols = slice(a * HALF_COLS, (a + 1) * HALF_COLS)
            kv_head[part] = kv_head_pool.tile([P, PACK, HALF_COLS], BF16, name="kv_head")
            for u in range(2):
                nc.sync.dma_start(
                    out=kv_head[part][:, 2 * u : 2 * u + 2, :], in_=kv_part_rows[0, c, :, u, :, cols]
                )

        def load_kv(half):
            b, c = divmod(half, PASSES)
            kv_raw[half] = kv_raw_pool.tile([P, PACK, FEATS], BF16, name="kv_raw")
            nc.sync.dma_start(
                out=kv_raw[half][:].rearrange("p (u e) w -> p u (e w)", e=2), in_=kv_rows[b, c]
            )

        def load_tokens(tiles, pool, rows, g, name, first=0, count=GROUP):
            b, start = divmod(g * GROUP, TILES)
            if g not in tiles:
                tiles[g] = pool.tile([P, GROUP, FEATS], BF16, name=name)
            nc.sync.dma_start(
                out=tiles[g][:, first : first + count, :],
                in_=rows[b, :, start + first : start + first + count, :],
            )

        def first_loads():
            load_kv_part(0)
            load_kv_part(1)
            load_tokens(q_nat, q_pool, q_rows, 0, "q_nat", 0, PAIR)
            load_kv_part(2)
            load_tokens(q_nat, q_pool, q_rows, 0, "q_nat", PAIR, PAIR)
            load_kv_part(3)
            load_tokens(v_nat, v_pool, v_rows, 0, "v_nat", 0, PAIR)
            load_tokens(q_nat, q_pool, q_rows, 1, "q_nat", 0, PAIR)
            load_kv(2)
            load_tokens(q_nat, q_pool, q_rows, 1, "q_nat", PAIR, PAIR)
            load_tokens(v_nat, v_pool, v_rows, 0, "v_nat", PAIR, PAIR)
            nc.sync.dma_start(out=bias[:], in_=b_proj.partition_broadcast(P))
            load_kv(3)
            load_tokens(q_nat, q_pool, q_rows, 2, "q_nat", 0, PAIR)
            nc.sync.dma_start(
                out=w_raw[:].rearrange("p c (u e) n -> p (c u) (e n)", e=2), in_=w_rows
            )
            load_tokens(q_nat, q_pool, q_rows, 2, "q_nat", PAIR, PAIR)
            load_tokens(v_nat, v_pool, v_rows, 1, "v_nat")
            load_kv(4)

        def later_loads(g):
            if g < N_GROUPS:
                load_tokens(q_nat, q_pool, q_rows, g, "q_nat")
            if g <= N_GROUPS:
                load_tokens(v_nat, v_pool, v_rows, g - 1, "v_nat")
            if g + 2 < N_GROUPS:
                load_kv(g + 2)

        def regroup_piece(k, copy, pool):
            part, i = divmod(k, HALF_COLS // PIECE_COLS)
            if part < KV_PARTS:
                source = kv_head[part][:, :, i * PIECE_COLS : (i + 1) * PIECE_COLS]
            else:
                half, a = divmod(k, FEATS // PIECE_COLS)
                source = kv_raw[half][:, :, a * PIECE_COLS : (a + 1) * PIECE_COLS]
            if i == 0:
                kv_grp[part] = pool.tile([P, HALF_COLS, PACK], BF16, name="kv_part", align_bytes=64)
            copy(
                out=kv_grp[part][:, i * PIECE_COLS : (i + 1) * PIECE_COLS, :].rearrange(
                    "p (c i) t -> p c t i", i=RUN
                ),
                in_=source.rearrange("p t (c i) -> p c t i", i=RUN),
            )

        def regroup_part(k):
            if k >= BATCH * KV_PARTS:
                return
            half, a = divmod(k, FEATS // HALF_COLS)
            kv_grp[k] = part_pool.tile([P, HALF_COLS, PACK], BF16, name="kv_part", align_bytes=64)
            cols = slice(a * HALF_COLS, a * HALF_COLS + GPSIMD_COLS)
            nc.gpsimd.tensor_scalar(
                out=kv_grp[k][:, :GPSIMD_COLS],
                in0=kv_raw[half][:, :, cols].rearrange("p t m -> p m t"),
                scalar1=1.0,
                scalar2=0.0,
                op0=ALU.mult,
                op1=ALU.add,
            )

        def regroup_rest(k):
            if k >= BATCH * KV_PARTS:
                return
            half, a = divmod(k, FEATS // HALF_COLS)
            cols = slice(a * HALF_COLS + GPSIMD_COLS, (a + 1) * HALF_COLS)
            nc.scalar.copy(
                out=kv_grp[k][:, GPSIMD_COLS:].rearrange("p (c i) t -> p c t i", i=RUN),
                in_=kv_raw[half][:, :, cols].rearrange("p t (c i) -> p c t i", i=RUN),
            )

        def quantise_kv(k):
            if not 0 <= k < BATCH * KV_PARTS:
                return
            b, ca = divmod(k, KV_PARTS)
            c, a = divmod(ca, FEATS // HALF_COLS)
            if ca == 0:
                kv_codes[b] = kv_pool.tile([P, PASSES, FEATS], U32, name="kv_codes", align_bytes=64)
                kv_scales[b] = kv_pool.tile([P, PASSES, FEATS], U8, name="kv_scales", align_bytes=64)
            cols = slice(a * HALF_COLS, (a + 1) * HALF_COLS)
            nc.vector.quantize_mx(
                out=kv_codes[b][:, c, cols].bitcast(FP8X4),
                scales=kv_scales[b][:, c, cols],
                in_=kv_grp[k][:].rearrange("p m t -> p (m t)"),
            )

        def regroup_w(c):
            nc.vector.tensor_copy(out=w_grp[:, c], in_=w_raw[:, c].rearrange("p t n -> p n t"))

        def quantise_w():
            nc.vector.quantize_mx(
                out=w_codes[:].rearrange("p c n -> p (c n)").bitcast(FP8X4),
                scales=w_scales[:].rearrange("p c n -> p (c n)"),
                in_=w_grp[:].rearrange("p c n t -> p (c n t)"),
            )

        def pair_tiles(p):
            return range(p * PAIR, (p + 1) * PAIR) if 0 <= p < N_PAIRS else ()

        def sum_squares(n):
            if not 0 <= n < N_TILES:
                return
            g, i = divmod(n, GROUP)
            p, j = divmod(n, PAIR)
            if j == 0:
                sumsq[p] = work.tile([P, PAIR], F32, name="sumsq")
            squares = work.tile([P, FEATS], BF16, name="squares")
            nc.scalar.activation(
                out=squares[:],
                in_=q_nat[g][:, i, :],
                func=ACT.Square,
                accum_out=sumsq[p][:, j : j + 1],
            )

        def floor_squares(p):
            if 0 <= p < N_PAIRS:
                excess[p] = work.tile([P, PAIR], F32, name="excess")
                nc.scalar.activation(out=excess[p][:], in_=sumsq[p][:], func=ACT.Relu, bias=-EPS_SQUARED)

        def invert_norms(p):
            if 0 <= p < N_PAIRS:
                inv_norm[p] = work.tile([P, PAIR], F32, name="inv_norm")
                nc.scalar.activation(
                    out=inv_norm[p][:], in_=excess[p][:], func=ACT.Abs_reciprocal_sqrt, bias=EPS_SQUARED
                )

        def normalise(n):
            if not 0 <= n < N_TILES:
                return
            g, i = divmod(n, GROUP)
            p, half = divmod(n, PAIR)
            if half == 0:
                q2_nat[p] = work.tile([P, PAIR, FEATS], BF16, name="q2_nat")
            nc.vector.tensor_scalar_mul(
                out=q2_nat[p][:, half, :],
                in0=q_nat[g][:, i, :],
                scalar1=inv_norm[p][:, half : half + 1],
            )

        def turn(natural):
            words = natural.bitcast(F32)
            bank = turn_psum.tile([P, WORD_BLOCKS, P], F32, name="turn_bank")
            for block in range(WORD_BLOCKS):
                nc.tensor.transpose(
                    out=bank[:, block, :], in_=words[:, block * P : (block + 1) * P], identity=ident[:]
                )
            return bank

        def copy_turned(bank, grouped):
            nc.scalar.copy(
                out=grouped.bitcast(F32), in_=bank[:].rearrange("p (c u) k -> p c k u", u=2)
            )

        def transpose_q2(p):
            for n in pair_tiles(p):
                q2_bank[n] = turn(q2_nat[p][:, n % PAIR, :])

        def copy_q2(n):
            if not 0 <= n < N_TILES:
                return
            p, half = divmod(n, PAIR)
            if half == 0:
                q2_grp[p] = work.tile([P, PAIR, PASSES, P, PACK], BF16, name="q2_grp", align_bytes=64)
            copy_turned(q2_bank[n], q2_grp[p][:, half])

        def transpose_h(n):
            h_bank[n] = turn(h_nat[n // PAIR][:, n % PAIR, :])

        def copy_h(n):
            p, half = divmod(n, PAIR)
            if half == 0:
                hT_grp[p] = work.tile([P, PAIR, PASSES, P, PACK], BF16, name="hT_grp", align_bytes=64)
            copy_turned(h_bank[n], hT_grp[p][:, half])

        def code_tiles(name):
            codes = work.tile([P, PAIR, PASSES, P], U32, name=name + "_codes", align_bytes=64)
            scales = work.tile([P, PAIR, PASSES, P], U8, name=name + "_scales", align_bytes=64)
            return codes, scales

        def quantise_tokens(codes, scales, grouped):
            nc.vector.quantize_mx(
                out=codes.rearrange("p n c k -> p (n c k)").bitcast(FP8X4),
                scales=scales.rearrange("p n c k -> p (n c k)"),
                in_=grouped.rearrange("p n c k t -> p (n c k t)"),
            )

        def quantise_q2(p):
            if 0 <= p < N_PAIRS:
                q2_codes[p], q2_scales[p] = code_tiles("q2")
                quantise_tokens(q2_codes[p][:], q2_scales[p][:], q2_grp[p][:])

        def quantise_h(p, first=0, count=PAIR):
            if 0 <= p < N_PAIRS:
                if first == 0:
                    h_codes[p], h_scales[p] = code_tiles("h")
                tiles = slice(first, first + count)
                quantise_tokens(h_codes[p][:, tiles], h_scales[p][:, tiles], hT_grp[p][:, tiles])

        def readout(n):
            if 0 <= n < N_TILES:
                p, b = n // PAIR, n // TILES
                for half in range(HALVES):
                    t2_bank[n, half] = t2_psum.tile([P, BANK_COLS], F32, name="t2_bank")
                    cols = slice(half * BANK_COLS, (half + 1) * BANK_COLS)
                    for c in range(PASSES):
                        nc.tensor.matmul_mx(
                            out=t2_bank[n, half][:],
                            lhsT=q2_codes[p][:, n % PAIR, c, :].bitcast(FP8X4),
                            lhsT_scale=q2_scales[p][:, n % PAIR, c, :],
                            rhs=kv_codes[b][:, c, cols].bitcast(FP8X4),
                            rhs_scale=kv_scales[b][:, c, cols],
                            start=(c == 0),
                            stop=(c == PASSES - 1),
                        )

        def add_values(n):
            g, i = divmod(n, GROUP)
            p, j = divmod(n, PAIR)
            if j == 0:
                h_nat[p] = work.tile([P, PAIR, FEATS], BF16, name="h_nat")
            for half in range(HALVES):
                cols = slice(half * BANK_COLS, (half + 1) * BANK_COLS)
                nc.vector.scalar_tensor_tensor(
                    out=h_nat[p][:, j, cols],
                    in0=t2_bank[n, half][:],
                    scalar=1.0 / math.sqrt(TOKENS),
                    in1=v_nat[g][:, i, cols],
                    op0=ALU.mult,
                    op1=ALU.add,
                )

        def project(n):
            p, half = divmod(n, PAIR)
            if half == 0 and p < N_PAIRS - 2:
                out_bank[p] = out_psum.tile([P, PAIR, OUT_FEATS], F32, name="out_bank")
            elif half == 0:
                out_bank[p] = t2_psum.tile([P, PAIR, OUT_FEATS], F32, name="t2_bank")
            for c2 in range(PASSES):
                nc.tensor.matmul_mx(
                    out=out_bank[p][:, half, :],
                    lhsT=h_codes[p][:, half, c2, :].bitcast(FP8X4),
                    lhsT_scale=h_scales[p][:, half, c2, :],
                    rhs=w_codes[:, c2, :].bitcast(FP8X4),
                    rhs_scale=w_scales[:, c2, :],
                    start=(c2 == 0),
                    stop=(c2 == PASSES - 1),
                )

        def add_bias(p, first=0, count=PAIR):
            if not 0 <= p < N_PAIRS:
                return
            if first == 0:
                out_sb[p] = out_pool.tile([P, PAIR, OUT_FEATS], F32, name="out_sb")
            tiles = slice(first, first + count)
            nc.vector.tensor_tensor(
                out=out_sb[p][:, tiles],
                in0=out_bank[p][:, tiles],
                in1=bias[:].unsqueeze(1).to_broadcast([P, count, OUT_FEATS]),
                op=ALU.add,
            )
            b, start = divmod(p * PAIR, TILES)
            nc.sync.dma_start(
                out=out_rows[b, :, start + first : start + first + count, :], in_=out_sb[p][:, tiles]
            )

        ctx.enter_context(tc.manual_schedule())
        vec, sca = nc.vector.tensor_copy, nc.scalar.copy

        first_loads()
        regroup_piece(0, vec, first_pool)
        regroup_piece(1, sca, first_pool)
        regroup_piece(2, sca, first_pool)
        regroup_piece(3, vec, first_pool)
        sum_squares(0)
        sum_squares(1)
        floor_squares(0)
        invert_norms(0)
        quantise_kv(0)
        regroup_piece(4, vec, first_pool)
        quantise_kv(1)
        regroup_piece(5, vec, first_pool)
        normalise(0)
        normalise(1)
        transpose_q2(0)
        regroup_piece(6, vec, part_pool)
        sum_squares(2)
        sum_squares(3)
        floor_squares(1)
        copy_q2(0)
        invert_norms(1)
        copy_q2(1)
        regroup_piece(7, vec, part_pool)
        quantise_kv(2)
        normalise(2)
        normalise(3)
        transpose_q2(1)
        quantise_q2(0)
        quantise_kv(3)
        regroup_part(KV_PARTS + 1)
        readout(0)
        readout(1)
        sum_squares(4)
        sum_squares(5)
        floor_squares(2)
        copy_q2(2)
        invert_norms(2)
        copy_q2(3)

        for s in range(N_PAIRS - 1):
            if s > 0 and s % 2 == 0:
                later_loads(s // 2 + 2)
            add_bias(s - 3)
            if s > 0:
                transpose_q2(s + 2)
            for n in pair_tiles(s - 2):
                project(n)
            for n in pair_tiles(s):
                add_values(n)
            if s == 0:
                regroup_piece(8, sca, first_pool)
            for n in pair_tiles(s + 3):
                sum_squares(n)
            if s == 0:
                normalise(4)
                normalise(5)
                transpose_q2(2)
            floor_squares(s + 3)
            copy_q2((s + 2) * PAIR)
            invert_norms(s + 3)
            copy_q2((s + 2) * PAIR + 1)
            regroup_rest(s + KV_PARTS + 1)
            if s == 0:
                quantise_q2(1)
                regroup_piece(9, vec, first_pool)
                quantise_kv(KV_PARTS)
            else:
                quantise_q2(s + 1)
            for n in pair_tiles(s):
                transpose_h(n)
                copy_h(n)
            for n in pair_tiles(s + 1):
                readout(n)
            if s == 1:
                regroup_w(0)
                regroup_w(1)
            normalise((s + 3) * PAIR)
            normalise((s + 3) * PAIR + 1)
            if s == 1:
                quantise_w()
            quantise_kv(s + KV_PARTS + 1)
            regroup_part(s + KV_PARTS + 2)
            quantise_h(s - 1)
        last = N_PAIRS - 1
        first, second = pair_tiles(last)
        add_bias(last - 3)
        for n in pair_tiles(last - 2):
            project(n)
        add_values(first)
        transpose_h(first)
        copy_h(first)
        add_values(second)
        transpose_h(second)
        copy_h(second)
        quantise_h(last - 1)
        add_bias(last - 2)
        for n in pair_tiles(last - 1):
            project(n)
        quantise_h(last, 0, 1)
        quantise_h(last, 1, 1)
        add_bias(last - 1)
        project(first)
        add_bias(last, 0, 1)
        project(second)
        add_bias(last, 1, 1)
